import numpy as np
import ml_dtypes


def mxq(x, axis, fmt="e4m3"):
    dtype, down = {"e4m3": (ml_dtypes.float8_e4m3fn, 7), "e5m2": (ml_dtypes.float8_e5m2, 14)}[fmt]
    v = np.moveaxis(np.asarray(x, np.float32).astype(ml_dtypes.bfloat16).astype(np.float64), axis, -1)
    blocks = v.reshape(v.shape[:-1] + (-1, 32))
    amax = np.abs(blocks).max(-1, keepdims=True)
    byte = np.maximum(np.where(amax > 0, np.frexp(amax)[1] - 1 + 127, 0) - down, 1)
    scale = np.exp2(byte - 127.0)
    codes = (blocks / scale).astype(np.float32).astype(dtype).astype(np.float64)
    return np.moveaxis((codes * scale).reshape(v.shape), -1, axis)


WIDE = False


def mx_kscale(k):
    if not WIDE:
        return np.ones(k)
    levels = np.array([10, -10, 5, -5, 0])
    a = np.random.permutation(np.resize(levels, k // 512 * 4)).reshape(k // 512, 4)
    idx = np.arange(k)
    return np.exp2(a[idx // 512, idx % 128 // 32])


BF16 = ml_dtypes.bfloat16


def bf(x):
    return np.asarray(x, np.float32).astype(BF16)


def f64(x):
    return np.asarray(x).astype(np.float64)


B, C, HID, FH, FW, PH, PW = 2, 512, 1536, 2, 2, 8, 16
EPS = 1e-5
H, WD = FH * PH, FW * PW
N1, N2, N3 = HID * C, HID * 9, C * HID


def relu6(v):
    return np.clip(v, 0.0, 6.0)


def bn(v, g, b, m, var):
    inv = g / np.sqrt(var + EPS)
    return v * inv[None, :, None, None] + (b - m * inv)[None, :, None, None]


def patch_pw(v, W):
    ci, co = v.shape[1], W.shape[3]
    vq = mxq(v, 1, 'e4m3')
    vb = vq.reshape(B, ci, FH, PH, FW, PW).transpose(0, 2, 4, 1, 3, 5).reshape(B, FH, FW, ci, PH * PW)
    y = mxq(W, 4, 'e4m3') @ vb
    return y.reshape(B, FH, FW, co, PH, PW).transpose(0, 3, 1, 4, 2, 5).reshape(B, co, H, WD)


def patch_dw3(v, K):
    c = v.shape[1]
    vp = np.pad(v, ((0, 0), (0, 0), (1, 1), (1, 1)), mode='reflect')
    acc = np.zeros((B, c, FH, PH, FW, PW))
    for dy in range(3):
        for dx in range(3):
            vs = vp[:, :, dy:dy + H, dx:dx + WD].reshape(B, c, FH, PH, FW, PW)
            k = K[:, :, :, :, dy, dx].transpose(0, 3, 1, 2)
            acc = acc + vs * k[:, :, :, None, :, None]
    return acc.reshape(B, c, H, WD)


def setup_inputs():
    s = mx_kscale(C)
    w1 = np.random.standard_normal((B, HID, C, FH, FW)) * 3.0 / np.sqrt(C) / s[None, None, :, None, None]
    k2 = np.random.standard_normal((B, N2, FH, FW)) * 0.45
    w3 = np.random.standard_normal((B, N3, FH, FW)) * 0.5 / np.sqrt(HID)
    return {
        'x': bf(np.random.standard_normal((B, C, H, WD)) * s[None, :, None, None]),
        'w': bf(np.concatenate([w1.reshape(B, N1, FH, FW), k2, w3], axis=1)),
        'g1': bf(np.random.uniform(0.5, 1.5, HID)),
        'b1': bf(np.random.standard_normal(HID)),
        'm1': bf(np.random.standard_normal(HID)),
        'v1': bf(np.random.uniform(0.5, 1.5, HID)),
        'g2': bf(np.random.uniform(0.5, 1.5, HID)),
        'b2': bf(np.random.standard_normal(HID)),
        'm2': bf(np.random.standard_normal(HID)),
        'v2': bf(np.random.uniform(0.5, 1.5, HID)),
        'g3': bf(np.random.uniform(0.5, 1.5, C) * s),
        'b3': bf(np.random.standard_normal(C) * 0.5 * s),
        'm3': bf(np.random.standard_normal(C) * 0.5),
        'v3': bf(np.random.uniform(0.5, 1.5, C)),
    }


def reference(x, w, g1, b1, m1, v1, g2, b2, m2, v2, g3, b3, m3, v3):
    x = f64(x)
    wg = f64(w).transpose(0, 2, 3, 1)
    W1 = wg[..., :N1].reshape(B, FH, FW, HID, C)
    K2 = wg[..., N1:N1 + N2].reshape(B, FH, FW, HID, 3, 3)
    W3 = wg[..., N1 + N2:].reshape(B, FH, FW, C, HID)
    h = relu6(bn(patch_pw(x, W1), f64(g1), f64(b1), f64(m1), f64(v1)))
    h = relu6(bn(patch_dw3(h, K2), f64(g2), f64(b2), f64(m2), f64(v2)))
    h = bn(patch_pw(h, W3), f64(g3), f64(b3), f64(m3), f64(v3))
    return x + h

@@ -1,0 +1,335 @@
+from contextlib import ExitStack
+
+import concourse.mybir as mybir
+from concourse.masks import make_identity
+
+FP8X4 = mybir.dt.float8_e4m3fn_x4
+BF16 = mybir.dt.bfloat16
+F32 = mybir.dt.float32
+U32 = mybir.dt.uint32
+U8 = mybir.dt.uint8
+ACT = mybir.ActivationFunctionType
+ALU = mybir.AluOpType
+AX = mybir.AxisListType
+
+P = 128
+B, C, HID = 2, 512, 1536
+H, WD = 16, 32
+NPIX = H * WD
+N1, N2, N3 = HID * C, HID * 9, C * HID
+EPS = 1e-5
+NJ = HID // P
+NCT = C // P
+FLOPS = 2 * B * NPIX * (2 * HID * C + 9 * HID)
+
+
+def tile_hyperpatchinvertedresidual_kernel(
+    tc, x, w, g1, b1, m1, v1, g2, b2, m2, v2, g3, b3, m3, v3, out
+):
+    nc = tc.nc
+    with ExitStack() as ctx:
+        const = ctx.enter_context(tc.tile_pool(name="const", bufs=1))
+        raw1 = ctx.enter_context(tc.tile_pool(name="raw1", bufs=4))
+        raw3 = ctx.enter_context(tc.tile_pool(name="raw3", bufs=2))
+        grp = ctx.enter_context(tc.tile_pool(name="grp", bufs=4))
+        w1q = ctx.enter_context(tc.tile_pool(name="w1q", bufs=3))
+        hpool = ctx.enter_context(tc.tile_pool(name="hpool", bufs=4))
+        apool = ctx.enter_context(tc.tile_pool(name="apool", bufs=2))
+        hgpool = ctx.enter_context(tc.tile_pool(name="hgpool", bufs=2))
+        opool = ctx.enter_context(tc.tile_pool(name="opool", bufs=3))
+        pst = ctx.enter_context(tc.psum_pool(name="pst", bufs=3))
+        psa = ctx.enter_context(tc.psum_pool(name="psa", bufs=2))
+        pse = ctx.enter_context(tc.psum_pool(name="pse", bufs=2))
+
+        w1v = [
+            w[b, 0:N1].rearrange("(j a q c) f g -> q j a (c f g)", j=NJ, a=4, q=P)
+            for b in range(B)
+        ]
+        w3v = [
+            w[b, N1 + N2 : N1 + N2 + N3].rearrange(
+                "(m q s o) f g -> q m (s o f g)", m=16, q=P, s=3
+            )
+            for b in range(B)
+        ]
+        k2v = [
+            w[b, N1 : N1 + N2].rearrange("(j p t) f g -> p j (t f g)", p=P, t=9)
+            for b in range(B)
+        ]
+
+        a_order = [(b, s0, t) for b in range(B) for s0 in range(3) for t in range(4)]
+        c_order = [(b, ct, s0) for b in range(B) for ct in range(NCT) for s0 in range(3)]
+
+        t1_tiles = {}
+        t3_tiles = {}
+
+        def load_w1(i):
+            b, s0, t = a_order[i]
+            t1 = raw1.tile([P, 4, 512], BF16, name="t1")
+            nc.sync.dma_start(out=t1[:], in_=w1v[b][:, 3 * t + s0])
+            t1_tiles[i] = t1
+
+        def load_w3(k):
+            b, ct = k // NCT, k % NCT
+            t3 = raw3.tile([P, 4, 1536], BF16, name="t3")
+            nc.sync.dma_start(out=t3[:], in_=w3v[b][:, 4 * ct : 4 * ct + 4])
+            t3_tiles[k] = t3
+
+        xraw = [const.tile([P, 4, NPIX], BF16, name="xraw%d" % b) for b in range(B)]
+        load_w1(0)
+        nc.sync.dma_start(
+            out=xraw[0][:], in_=x[0].rearrange("(t p) y z -> p t (y z)", p=P)
+        )
+
+        ident = const.tile([P, P], BF16, name="ident")
+        make_identity(nc, ident[:])
+        six = const.tile([P, 1], F32, name="six")
+        nc.vector.memset(six[:], 6.0)
+        warm = const.tile([P, 1], F32, name="warm")
+        nc.scalar.sqrt(out=warm[:], in_=six[:])
+
+        praw = const.tile([P, P], BF16, name="praw")
+        nc.vector.memset(praw[:], 0.0)
+        rows = [
+            (g1, 0, NJ), (g2, 12, NJ), (g3, 24, NCT),
+            (b1, 28, NJ), (b2, 40, NJ), (b3, 52, NCT),
+            (m1, 56, NJ), (m2, 68, NJ), (m3, 80, NCT),
+            (v1, 84, NJ), (v2, 96, NJ), (v3, 108, NCT),
+        ]
+        for vec, r0, n in rows:
+            nc.scalar.dma_start(
+                out=praw[r0 : r0 + n, :], in_=vec.rearrange("(j e) -> j e", e=P)
+            )
+        k2raw = [const.tile([P, NJ, 36], BF16, name="k2raw%d" % b) for b in range(B)]
+        for b in range(B):
+            nc.scalar.dma_start(out=k2raw[b][:], in_=k2v[b])
+        load_w1(1)
+        load_w1(2)
+        load_w3(0)
+        nc.sync.dma_start(
+            out=xraw[1][:], in_=x[1].rearrange("(t p) y z -> p t (y z)", p=P)
+        )
+
+        pf = const.tile([P, 112], F32, name="pf")
+        ve = const.tile([P, 28], F32, name="ve")
+        sd = const.tile([P, 28], F32, name="sd")
+        rsd = const.tile([P, 28], F32, name="rsd")
+        inv = const.tile([P, 28], F32, name="inv")
+        mi = const.tile([P, 28], F32, name="mi")
+        beta = const.tile([P, 28], F32, name="beta")
+        ninv2 = const.tile([P, NJ], F32, name="ninv2")
+
+        def prep_bn():
+            ptp = pst.tile([P, 1024], BF16, name="tp")
+            nc.tensor.transpose(ptp[:, 0:P], praw[:], ident[:])
+            nc.vector.tensor_copy(out=pf[:], in_=ptp[:, 0:112])
+            nc.vector.tensor_scalar_add(out=ve[:], in0=pf[:, 84:112], scalar1=EPS)
+            nc.scalar.sqrt(out=sd[:], in_=ve[:])
+            nc.vector.reciprocal(out=rsd[:], in_=sd[:])
+            nc.vector.tensor_mul(out=inv[:], in0=pf[:, 0:28], in1=rsd[:])
+            nc.vector.tensor_mul(out=mi[:], in0=pf[:, 56:84], in1=inv[:])
+            nc.vector.tensor_sub(out=beta[:], in0=pf[:, 28:56], in1=mi[:])
+            nc.vector.tensor_scalar_mul(out=ninv2[:], in0=inv[:, 12:24], scalar1=-1.0)
+
+        xc = [const.tile([P, NPIX], U32, name="xc%d" % b, align_bytes=64) for b in range(B)]
+        xs = [const.tile([P, NPIX], U8, name="xs%d" % b, align_bytes=64) for b in range(B)]
+        xb = [const.tile([P, NCT, NPIX], F32, name="xb%d" % b) for b in range(B)]
+
+        def prep_x(b):
+            xg = grp.tile([P, 2048], BF16, name="g", align_bytes=64)
+            xgv = xg[:].rearrange("p (g y z t) -> p g y z t", g=2, y=H, z=16)
+            xrv = xraw[b][:].rearrange("p t (y g z) -> p g y z t", y=H, g=2)
+            for g_ in range(2):
+                nc.vector.tensor_copy(out=xgv[:, g_], in_=xrv[:, g_])
+            nc.vector.quantize_mx(out=xc[b][:].bitcast(FP8X4), scales=xs[b][:], in_=xg[:])
+
+        def prep_xb(b):
+            for ct in range(NCT):
+                nc.scalar.activation(
+                    out=xb[b][:, ct, :], in_=xraw[b][:, ct, :], func=ACT.Identity,
+                    bias=beta[:, 24 + ct : 25 + ct], scale=1.0,
+                )
+
+        k2f = [const.tile([P, NJ, 36], F32, name="k2f%d" % b) for b in range(B)]
+        ksum = [const.tile([P, NJ, 4], F32, name="ksum%d" % b) for b in range(B)]
+        bias2 = [const.tile([P, NJ, 4], F32, name="bias2%d" % b) for b in range(B)]
+
+        def prep_k2(b):
+            nc.vector.tensor_tensor(
+                out=k2f[b][:], in0=k2raw[b][:],
+                in1=ninv2[:].unsqueeze(2).to_broadcast([P, NJ, 36]), op=ALU.mult,
+            )
+            nc.vector.tensor_reduce(
+                out=ksum[b][:], in_=k2f[b][:].rearrange("p j (t e) -> p j e t", e=4),
+                axis=AX.X, op=ALU.add,
+            )
+            nc.vector.scalar_tensor_tensor(
+                out=bias2[b][:], in0=ksum[b][:], scalar=-6.0,
+                in1=beta[:, 12:24].unsqueeze(2).to_broadcast([P, NJ, 4]),
+                op0=ALU.mult, op1=ALU.add,
+            )
+
+        def fg_of(pi):
+            return 2 * (pi % 2) + pi // 2
+
+        def prep_w(src_of, codes, scales):
+            g = grp.tile([P, 2048], BF16, name="g", align_bytes=64)
+            for half in range(2):
+                tp = pst.tile([P, 1024], BF16, name="tp")
+                for k in range(8):
+                    pi, a = 2 * half + k // 4, k % 4
+                    nc.tensor.transpose(tp[:, k * P : (k + 1) * P], src_of(pi, a), ident[:])
+                nc.scalar.copy(out=g[:, half * 1024 : (half + 1) * 1024], in_=tp[:])
+            nc.vector.quantize_mx(out=codes.bitcast(FP8X4), scales=scales, in_=g[:])
+
+        w1c_t = {}
+        w1s_t = {}
+
+        def prep_a(i):
+            t1 = t1_tiles[i]
+            w1c = w1q.tile([P, 512], U32, name="w1c", align_bytes=64)
+            w1s = w1q.tile([P, 512], U8, name="w1s", align_bytes=64)
+
+            def src_of(pi, a):
+                return t1[:, a, :].rearrange("q (c e) -> q c e", e=4)[:, :, fg_of(pi)]
+
+            prep_w(src_of, w1c[:], w1s[:])
+            w1c_t[i], w1s_t[i] = w1c, w1s
+
+        w3c = [const.tile([P, 12, 512], U32, name="w3c%d" % b, align_bytes=64) for b in range(B)]
+        w3s = [const.tile([P, 12, 512], U8, name="w3s%d" % b, align_bytes=64) for b in range(B)]
+
+        def prep_c(i):
+            b, ct, s0 = c_order[i]
+            if s0 == 0 and b * NCT + ct + 1 < B * NCT:
+                load_w3(b * NCT + ct + 1)
+            t3 = t3_tiles[b * NCT + ct]
+
+            def src_of(pi, a):
+                return t3[:, a, :].rearrange("q (s o e) -> q s o e", s=3, e=4)[
+                    :, s0, :, fg_of(pi)
+                ]
+
+            u = ct * 3 + s0
+            prep_w(src_of, w3c[b][:, u, :], w3s[b][:, u, :])
+
+        hp_t = {}
+        acc_t = {}
+
+        def win(hp, pi, dy, dx):
+            g_, f_ = pi // 2, pi % 2
+            return hp[:, 8 * f_ + dy : 8 * f_ + dy + 8, 16 * g_ + dx : 16 * g_ + dx + 16]
+
+        def accv(acc, t, pi):
+            return acc[:, t, pi * P : (pi + 1) * P].rearrange("p (y z) -> p y z", y=8)
+
+        def front(i):
+            b, s0, t = a_order[i]
+            j = 3 * t + s0
+            a1 = psa.tile([P, NPIX], F32, name="a1")
+            for pi in range(4):
+                cols = slice(pi * P, (pi + 1) * P)
+                nc.tensor.matmul_mx(
+                    out=a1[:, cols],
+                    lhsT=w1c_t[i][:, cols].bitcast(FP8X4), lhsT_scale=w1s_t[i][:, cols],
+                    rhs=xc[b][:, cols].bitcast(FP8X4), rhs_scale=xs[b][:, cols],
+                    start=True, stop=True,
+                )
+            hp = hpool.tile([P, H + 2, WD + 2], F32, name="hp")
+            inner = hp[:, 1 : H + 1, 1 : WD + 1]
+            nc.scalar.activation(
+                out=inner.rearrange("p y (g z) -> p g y z", g=2),
+                in_=a1[:].rearrange("p (g y z) -> p g y z", g=2, y=H),
+                func=ACT.Relu, bias=beta[:, j : j + 1], scale=inv[:, j : j + 1],
+            )
+            nc.scalar.activation(out=inner, in_=inner, func=ACT.Relu, bias=six[:], scale=-1.0)
+            nc.scalar.copy(out=hp[:, 1 : H + 1, 0 : WD + 2 : WD + 1], in_=hp[:, 1 : H + 1, 2:WD:29])
+            nc.scalar.copy(out=hp[:, 0 : H + 2 : H + 1, :], in_=hp[:, 2:H:13, :])
+            if t == 0:
+                acc_t[(b, s0)] = apool.tile([P, 4, NPIX], F32, name="acc")
+            acc = acc_t[(b, s0)]
+            for pi in range(4):
+                fg = fg_of(pi)
+                nc.scalar.activation(
+                    out=accv(acc, t, pi), in_=win(hp, pi, 0, 0), func=ACT.Identity,
+                    bias=bias2[b][:, j, fg : fg + 1], scale=k2f[b][:, j, fg : fg + 1],
+                )
+            hp_t[i] = hp
+
+        h2c = [const.tile([P, 3, NPIX], U32, name="h2c%d" % b, align_bytes=64) for b in range(B)]
+        h2s = [const.tile([P, 3, NPIX], U8, name="h2s%d" % b, align_bytes=64) for b in range(B)]
+
+        def depthwise(i):
+            b, s0, t = a_order[i]
+            j = 3 * t + s0
+            hp, acc = hp_t[i], acc_t[(b, s0)]
+            for tap in range(1, 9):
+                for pi in range(4):
+                    k = tap * 4 + fg_of(pi)
+                    nc.vector.scalar_tensor_tensor(
+                        out=accv(acc, t, pi), in0=win(hp, pi, tap // 3, tap % 3),
+                        scalar=k2f[b][:, j, k : k + 1], in1=accv(acc, t, pi),
+                        op0=ALU.mult, op1=ALU.add,
+                    )
+            if t == 3:
+                h2g = hgpool.tile([P, NPIX, 4], BF16, name="h2g", align_bytes=64)
+                nc.vector.tensor_scalar(
+                    out=h2g[:], in0=acc[:].rearrange("p t n -> p n t"),
+                    scalar1=0.0, scalar2=6.0, op0=ALU.max, op1=ALU.min,
+                )
+                nc.vector.quantize_mx(
+                    out=h2c[b][:, s0, :].bitcast(FP8X4), scales=h2s[b][:, s0, :],
+                    in_=h2g[:].rearrange("p n t -> p (n t)"),
+                )
+
+        def step3(b):
+            for ct in range(NCT):
+                e3 = pse.tile([P, NPIX], F32, name="e3")
+                for pi in range(4):
+                    cols = slice(pi * P, (pi + 1) * P)
+                    for s0 in range(3):
+                        u = ct * 3 + s0
+                        nc.tensor.matmul_mx(
+                            out=e3[:, cols],
+                            lhsT=w3c[b][:, u, cols].bitcast(FP8X4), lhsT_scale=w3s[b][:, u, cols],
+                            rhs=h2c[b][:, s0, cols].bitcast(FP8X4), rhs_scale=h2s[b][:, s0, cols],
+                            start=(s0 == 0), stop=(s0 == 2),
+                        )
+                ot = opool.tile([P, NPIX], F32, name="ot")
+                for g_ in range(2):
+                    nc.vector.scalar_tensor_tensor(
+                        out=ot[:].rearrange("p (y g z) -> p g y z", y=H, g=2)[:, g_],
+                        in0=e3[:, g_ * 256 : (g_ + 1) * 256].rearrange("p (y z) -> p y z", y=H),
+                        scalar=inv[:, 24 + ct : 25 + ct],
+                        in1=xb[b][:, ct, :].rearrange("p (y g z) -> p g y z", y=H, g=2)[:, g_],
+                        op0=ALU.mult, op1=ALU.add,
+                    )
+                nc.sync.dma_start(
+                    out=out[b, ct * P : (ct + 1) * P].rearrange("c y z -> c (y z)"), in_=ot[:]
+                )
+
+        n_a = len(a_order)
+        prep_x(0)
+        prep_a(0)
+        prep_bn()
+        prep_k2(0)
+        front(0)
+        prep_a(1)
+        for i in range(n_a):
+            if i + 3 < n_a:
+                load_w1(i + 3)
+            if i + 2 < n_a:
+                prep_a(i + 2)
+            if i + 1 < n_a:
+                front(i + 1)
+            prep_c(i)
+            if i == 2:
+                prep_xb(0)
+            if i == 6:
+                prep_x(1)
+                prep_k2(1)
+            if i == 14:
+                prep_xb(1)
+            depthwise(i)
+            if i == 11:
+                step3(0)
+        step3(1)

@@ -82,6 +82,8 @@ def tile_hyperpatchinvertedresidual_kernel(
 
         ident = const.tile([P, P], BF16, name="ident")
         make_identity(nc, ident[:])
+        identf = const.tile([P, P], F32, name="identf")
+        make_identity(nc, identf[:])
         six = const.tile([P, 1], F32, name="six")
         nc.vector.memset(six[:], 6.0)
         warm = const.tile([P, 1], F32, name="warm")
@@ -181,6 +183,18 @@ def tile_hyperpatchinvertedresidual_kernel(
                 nc.scalar.copy(out=g[:, half * 1024 : (half + 1) * 1024], in_=tp[:])
             nc.vector.quantize_mx(out=codes.bitcast(FP8X4), scales=scales, in_=g[:])
 
+        def prep_w_words(words_of, codes, scales):
+            g = grp.tile([P, 2048], BF16, name="g", align_bytes=64)
+            gv = g[:].rearrange("p (g f n) -> p f g n", g=2, f=2)
+            for f_ in range(2):
+                tp = pst.tile([P, 512], F32, name="tp")
+                for a in range(4):
+                    nc.tensor.transpose(tp[:, a * P : (a + 1) * P], words_of(f_, a), identf[:])
+                nc.scalar.copy(
+                    out=gv[:, f_], in_=tp[:].bitcast(BF16).rearrange("p (n g) -> p g n", g=2)
+                )
+            nc.vector.quantize_mx(out=codes.bitcast(FP8X4), scales=scales, in_=g[:])
+
         w1c_t = {}
         w1s_t = {}
 
@@ -189,10 +203,12 @@ def tile_hyperpatchinvertedresidual_kernel(
             w1c = w1q.tile([P, 512], U32, name="w1c", align_bytes=64)
             w1s = w1q.tile([P, 512], U8, name="w1s", align_bytes=64)
 
-            def src_of(pi, a):
-                return t1[:, a, :].rearrange("q (c e) -> q c e", e=4)[:, :, fg_of(pi)]
+            t1w = t1[:].bitcast(F32)
 
-            prep_w(src_of, w1c[:], w1s[:])
+            def words_of(f_, a):
+                return t1w[:, a, f_:256:2]
+
+            prep_w_words(words_of, w1c[:], w1s[:])
             w1c_t[i], w1s_t[i] = w1c, w1s
 
         w3c = [const.tile([P, 12, 512], U32, name="w3c%d" % b, align_bytes=64) for b in range(B)]

@@ -28,15 +28,15 @@ def tile_hyperpatchinvertedresidual_kernel(
 ):
     nc = tc.nc
     with ExitStack() as ctx:
+        ctx.enter_context(tc.manual_schedule())
         const = ctx.enter_context(tc.tile_pool(name="const", bufs=1))
-        raw1 = ctx.enter_context(tc.tile_pool(name="raw1", bufs=4))
+        raw1 = ctx.enter_context(tc.tile_pool(name="raw1", bufs=5))
         raw3 = ctx.enter_context(tc.tile_pool(name="raw3", bufs=2))
         grp = ctx.enter_context(tc.tile_pool(name="grp", bufs=4))
         w1q = ctx.enter_context(tc.tile_pool(name="w1q", bufs=3))
         hpool = ctx.enter_context(tc.tile_pool(name="hpool", bufs=4))
         apool = ctx.enter_context(tc.tile_pool(name="apool", bufs=2))
         hgpool = ctx.enter_context(tc.tile_pool(name="hgpool", bufs=2))
-        opool = ctx.enter_context(tc.tile_pool(name="opool", bufs=3))
         pst = ctx.enter_context(tc.psum_pool(name="pst", bufs=3))
         psa = ctx.enter_context(tc.psum_pool(name="psa", bufs=2))
         pse = ctx.enter_context(tc.psum_pool(name="pse", bufs=2))
@@ -55,101 +55,122 @@ def tile_hyperpatchinvertedresidual_kernel(
             w[b, N1 : N1 + N2].rearrange("(j p t) f g -> p j (t f g)", p=P, t=9)
             for b in range(B)
         ]
+        outv = [out[b].rearrange("(ct p) y z -> p ct (y z)", p=P) for b in range(B)]
 
         a_order = [(b, s0, t) for b in range(B) for s0 in range(3) for t in range(4)]
         c_order = [(b, ct, s0) for b in range(B) for ct in range(NCT) for s0 in range(3)]
+        n_a = len(a_order)
 
         t1_tiles = {}
         t3_tiles = {}
 
-        def load_w1(i):
+        def ld_a(i):
             b, s0, t = a_order[i]
             t1 = raw1.tile([P, 4, 512], BF16, name="t1")
             nc.sync.dma_start(out=t1[:], in_=w1v[b][:, 3 * t + s0])
             t1_tiles[i] = t1
 
-        def load_w3(k):
+        def ld_c(k):
             b, ct = k // NCT, k % NCT
             t3 = raw3.tile([P, 4, 1536], BF16, name="t3")
             nc.sync.dma_start(out=t3[:], in_=w3v[b][:, 4 * ct : 4 * ct + 4])
             t3_tiles[k] = t3
 
         xraw = [const.tile([P, 4, NPIX], BF16, name="xraw%d" % b) for b in range(B)]
-        load_w1(0)
-        nc.sync.dma_start(
-            out=xraw[0][:], in_=x[0].rearrange("(t p) y z -> p t (y z)", p=P)
-        )
 
-        ident = const.tile([P, P], BF16, name="ident")
-        make_identity(nc, ident[:])
-        identf = const.tile([P, P], F32, name="identf")
-        make_identity(nc, identf[:])
+        def ld_x(b):
+            nc.sync.dma_start(out=xraw[b][:], in_=x[b].rearrange("(t p) y z -> p t (y z)", p=P))
+
         six = const.tile([P, 1], F32, name="six")
         nc.vector.memset(six[:], 6.0)
+        praw = const.tile([P, P], BF16, name="praw")
+        nc.vector.memset(praw[:], 0.0)
+        praw3 = const.tile([P, P], BF16, name="praw3")
+        nc.vector.memset(praw3[:], 0.0)
+
+        def ld_vec(eng, dst, vec, r0, n):
+            eng.dma_start(out=dst[r0 : r0 + n, :], in_=vec.rearrange("(j e) -> j e", e=P))
+
+        k2raw = [const.tile([P, NJ, 36], BF16, name="k2raw%d" % b) for b in range(B)]
+        ld_a(0)
+        ld_x(0)
+        ld_vec(nc.scalar, praw, g1, 0, NJ)
+        ld_vec(nc.scalar, praw, v1, 72, NJ)
+        ld_vec(nc.scalar, praw, m1, 48, NJ)
+        ld_vec(nc.scalar, praw, b1, 24, NJ)
+        ld_vec(nc.scalar, praw, g2, 12, NJ)
+        ld_vec(nc.scalar, praw, v2, 84, NJ)
+        ld_vec(nc.gpsimd, praw, m2, 60, NJ)
+        ld_vec(nc.gpsimd, praw, b2, 36, NJ)
+        nc.gpsimd.dma_start(out=k2raw[0][:], in_=k2v[0])
+        identf = const.tile([P, P], F32, name="identf")
+        make_identity(nc, identf[:])
+        ident = const.tile([P, P], BF16, name="ident")
+        make_identity(nc, ident[:])
+        ld_a(1)
+        ld_x(1)
+        ld_a(2)
+        ld_c(0)
+        ld_a(3)
+        ld_vec(nc.sync, praw3, g3, 0, NCT)
+        ld_vec(nc.sync, praw3, v3, 12, NCT)
+        ld_vec(nc.sync, praw3, m3, 8, NCT)
+        ld_vec(nc.sync, praw3, b3, 4, NCT)
+        nc.sync.dma_start(out=k2raw[1][:], in_=k2v[1])
         warm = const.tile([P, 1], F32, name="warm")
         nc.scalar.sqrt(out=warm[:], in_=six[:])
 
-        praw = const.tile([P, P], BF16, name="praw")
-        nc.vector.memset(praw[:], 0.0)
-        rows = [
-            (g1, 0, NJ), (g2, 12, NJ), (g3, 24, NCT),
-            (b1, 28, NJ), (b2, 40, NJ), (b3, 52, NCT),
-            (m1, 56, NJ), (m2, 68, NJ), (m3, 80, NCT),
-            (v1, 84, NJ), (v2, 96, NJ), (v3, 108, NCT),
-        ]
-        for vec, r0, n in rows:
-            nc.scalar.dma_start(
-                out=praw[r0 : r0 + n, :], in_=vec.rearrange("(j e) -> j e", e=P)
-            )
-        k2raw = [const.tile([P, NJ, 36], BF16, name="k2raw%d" % b) for b in range(B)]
-        for b in range(B):
-            nc.scalar.dma_start(out=k2raw[b][:], in_=k2v[b])
-        load_w1(1)
-        load_w1(2)
-        load_w3(0)
-        nc.sync.dma_start(
-            out=xraw[1][:], in_=x[1].rearrange("(t p) y z -> p t (y z)", p=P)
-        )
-
-        pf = const.tile([P, 112], F32, name="pf")
-        ve = const.tile([P, 28], F32, name="ve")
-        sd = const.tile([P, 28], F32, name="sd")
-        rsd = const.tile([P, 28], F32, name="rsd")
-        inv = const.tile([P, 28], F32, name="inv")
-        mi = const.tile([P, 28], F32, name="mi")
-        beta = const.tile([P, 28], F32, name="beta")
+        inv = const.tile([P, 24], F32, name="inv")
+        beta = const.tile([P, 24], F32, name="beta")
+        inv3 = const.tile([P, NCT], F32, name="inv3")
+        beta3 = const.tile([P, NCT], F32, name="beta3")
         ninv2 = const.tile([P, NJ], F32, name="ninv2")
+        bn_tmp = {}
 
-        def prep_bn():
+        def bn_first(key, src, n):
             ptp = pst.tile([P, 1024], BF16, name="tp")
-            nc.tensor.transpose(ptp[:, 0:P], praw[:], ident[:])
-            nc.vector.tensor_copy(out=pf[:], in_=ptp[:, 0:112])
-            nc.vector.tensor_scalar_add(out=ve[:], in0=pf[:, 84:112], scalar1=EPS)
+            nc.tensor.transpose(ptp[:, 0:P], src[:], ident[:])
+            pf = const.tile([P, 4 * n], F32, name="pf" + key)
+            ve = const.tile([P, n], F32, name="ve" + key)
+            sd = const.tile([P, n], F32, name="sd" + key)
+            nc.vector.tensor_copy(out=pf[:], in_=ptp[:, 0 : 4 * n])
+            nc.vector.tensor_scalar_add(out=ve[:], in0=pf[:, 3 * n : 4 * n], scalar1=EPS)
             nc.scalar.sqrt(out=sd[:], in_=ve[:])
+            bn_tmp[key] = (pf, sd)
+
+        def bn_second(key, n, inv_o, beta_o):
+            pf, sd = bn_tmp[key]
+            rsd = const.tile([P, n], F32, name="rsd" + key)
+            mi = const.tile([P, n], F32, name="mi" + key)
             nc.vector.reciprocal(out=rsd[:], in_=sd[:])
-            nc.vector.tensor_mul(out=inv[:], in0=pf[:, 0:28], in1=rsd[:])
-            nc.vector.tensor_mul(out=mi[:], in0=pf[:, 56:84], in1=inv[:])
-            nc.vector.tensor_sub(out=beta[:], in0=pf[:, 28:56], in1=mi[:])
-            nc.vector.tensor_scalar_mul(out=ninv2[:], in0=inv[:, 12:24], scalar1=-1.0)
+            nc.vector.tensor_mul(out=inv_o[:], in0=pf[:, 0:n], in1=rsd[:])
+            nc.vector.tensor_mul(out=mi[:], in0=pf[:, 2 * n : 3 * n], in1=inv_o[:])
+            nc.vector.tensor_sub(out=beta_o[:], in0=pf[:, n : 2 * n], in1=mi[:])
 
         xc = [const.tile([P, NPIX], U32, name="xc%d" % b, align_bytes=64) for b in range(B)]
         xs = [const.tile([P, NPIX], U8, name="xs%d" % b, align_bytes=64) for b in range(B)]
         xb = [const.tile([P, NCT, NPIX], F32, name="xb%d" % b) for b in range(B)]
+        xg_t = {}
 
-        def prep_x(b):
+        def regroup_x(b, engs):
             xg = grp.tile([P, 2048], BF16, name="g", align_bytes=64)
             xgv = xg[:].rearrange("p (g y z t) -> p g y z t", g=2, y=H, z=16)
             xrv = xraw[b][:].rearrange("p t (y g z) -> p g y z t", y=H, g=2)
             for g_ in range(2):
-                nc.vector.tensor_copy(out=xgv[:, g_], in_=xrv[:, g_])
-            nc.vector.quantize_mx(out=xc[b][:].bitcast(FP8X4), scales=xs[b][:], in_=xg[:])
+                if engs[g_] == "v":
+                    nc.vector.tensor_copy(out=xgv[:, g_], in_=xrv[:, g_])
+                else:
+                    nc.scalar.copy(out=xgv[:, g_], in_=xrv[:, g_])
+            xg_t[b] = xg
 
-        def prep_xb(b):
-            for ct in range(NCT):
-                nc.scalar.activation(
-                    out=xb[b][:, ct, :], in_=xraw[b][:, ct, :], func=ACT.Identity,
-                    bias=beta[:, 24 + ct : 25 + ct], scale=1.0,
-                )
+        def q_x(b):
+            nc.vector.quantize_mx(out=xc[b][:].bitcast(FP8X4), scales=xs[b][:], in_=xg_t[b][:])
+
+        def prep_xb(b, ct):
+            nc.scalar.activation(
+                out=xb[b][:, ct, :], in_=xraw[b][:, ct, :], func=ACT.Identity,
+                bias=beta3[:, ct : ct + 1], scale=1.0,
+            )
 
         k2f = [const.tile([P, NJ, 36], F32, name="k2f%d" % b) for b in range(B)]
         ksum = [const.tile([P, NJ, 4], F32, name="ksum%d" % b) for b in range(B)]
@@ -173,61 +194,69 @@ def tile_hyperpatchinvertedresidual_kernel(
         def fg_of(pi):
             return 2 * (pi % 2) + pi // 2
 
-        def prep_w(src_of, codes, scales):
-            g = grp.tile([P, 2048], BF16, name="g", align_bytes=64)
-            for half in range(2):
-                tp = pst.tile([P, 1024], BF16, name="tp")
-                for k in range(8):
-                    pi, a = 2 * half + k // 4, k % 4
-                    nc.tensor.transpose(tp[:, k * P : (k + 1) * P], src_of(pi, a), ident[:])
-                nc.scalar.copy(out=g[:, half * 1024 : (half + 1) * 1024], in_=tp[:])
-            nc.vector.quantize_mx(out=codes.bitcast(FP8X4), scales=scales, in_=g[:])
+        ga_t = {}
+        gc_t = {}
+        w1c_t = {}
+        w1s_t = {}
 
-        def prep_w_words(words_of, codes, scales):
+        def t_a(i, vector_half=False):
             g = grp.tile([P, 2048], BF16, name="g", align_bytes=64)
+            ga_t[i] = g
+            if i % 2 == 1:
+                t1 = t1_tiles[i]
+                for half in range(2):
+                    tp = pst.tile([P, 1024], BF16, name="tp")
+                    for kk in range(8):
+                        pi, a = 2 * half + kk // 4, kk % 4
+                        src = t1[:, a, :].rearrange("q (c e) -> q c e", e=4)[:, :, fg_of(pi)]
+                        nc.tensor.transpose(tp[:, kk * P : (kk + 1) * P], src, ident[:])
+                    nc.scalar.copy(out=g[:, half * 1024 : (half + 1) * 1024], in_=tp[:])
+                return
+            t1w = t1_tiles[i][:].bitcast(F32)
             gv = g[:].rearrange("p (g f n) -> p f g n", g=2, f=2)
             for f_ in range(2):
                 tp = pst.tile([P, 512], F32, name="tp")
                 for a in range(4):
-                    nc.tensor.transpose(tp[:, a * P : (a + 1) * P], words_of(f_, a), identf[:])
-                nc.scalar.copy(
-                    out=gv[:, f_], in_=tp[:].bitcast(BF16).rearrange("p (n g) -> p g n", g=2)
-                )
-            nc.vector.quantize_mx(out=codes.bitcast(FP8X4), scales=scales, in_=g[:])
+                    nc.tensor.transpose(tp[:, a * P : (a + 1) * P], t1w[:, a, f_:256:2], identf[:])
+                src = tp[:].bitcast(BF16).rearrange("p (n g) -> p g n", g=2)
+                if vector_half and f_ == 1:
+                    nc.vector.tensor_copy(out=gv[:, f_], in_=src)
+                else:
+                    nc.scalar.copy(out=gv[:, f_], in_=src)
 
-        w1c_t = {}
-        w1s_t = {}
-
-        def prep_a(i):
-            t1 = t1_tiles[i]
+        def q_a(i):
             w1c = w1q.tile([P, 512], U32, name="w1c", align_bytes=64)
             w1s = w1q.tile([P, 512], U8, name="w1s", align_bytes=64)
-
-            t1w = t1[:].bitcast(F32)
-
-            def words_of(f_, a):
-                return t1w[:, a, f_:256:2]
-
-            prep_w_words(words_of, w1c[:], w1s[:])
+            nc.vector.quantize_mx(out=w1c[:].bitcast(FP8X4), scales=w1s[:], in_=ga_t[i][:])
             w1c_t[i], w1s_t[i] = w1c, w1s
 
         w3c = [const.tile([P, 12, 512], U32, name="w3c%d" % b, align_bytes=64) for b in range(B)]
         w3s = [const.tile([P, 12, 512], U8, name="w3s%d" % b, align_bytes=64) for b in range(B)]
 
-        def prep_c(i):
+        def t_c(i):
             b, ct, s0 = c_order[i]
-            if s0 == 0 and b * NCT + ct + 1 < B * NCT:
-                load_w3(b * NCT + ct + 1)
-            t3 = t3_tiles[b * NCT + ct]
+            k = b * NCT + ct
+            if s0 == 0 and k + 1 < B * NCT:
+                ld_c(k + 1)
+            t3 = t3_tiles[k]
+            g = grp.tile([P, 2048], BF16, name="g", align_bytes=64)
+            for half in range(2):
+                tp = pst.tile([P, 1024], BF16, name="tp")
+                for kk in range(8):
+                    pi, a = 2 * half + kk // 4, kk % 4
+                    src = t3[:, a, :].rearrange("q (s o e) -> q s o e", s=3, e=4)[:, s0, :, fg_of(pi)]
+                    nc.tensor.transpose(tp[:, kk * P : (kk + 1) * P], src, ident[:])
+                nc.scalar.copy(out=g[:, half * 1024 : (half + 1) * 1024], in_=tp[:])
+            gc_t[i] = g
 
-            def src_of(pi, a):
-                return t3[:, a, :].rearrange("q (s o e) -> q s o e", s=3, e=4)[
-                    :, s0, :, fg_of(pi)
-                ]
-
+        def q_c(i):
+            b, ct, s0 = c_order[i]
             u = ct * 3 + s0
-            prep_w(src_of, w3c[b][:, u, :], w3s[b][:, u, :])
+            nc.vector.quantize_mx(
+                out=w3c[b][:, u, :].bitcast(FP8X4), scales=w3s[b][:, u, :], in_=gc_t[i][:]
+            )
 
+        a1_t = {}
         hp_t = {}
         acc_t = {}
 
@@ -238,9 +267,8 @@ def tile_hyperpatchinvertedresidual_kernel(
         def accv(acc, t, pi):
             return acc[:, t, pi * P : (pi + 1) * P].rearrange("p (y z) -> p y z", y=8)
 
-        def front(i):
+        def mm_a(i):
             b, s0, t = a_order[i]
-            j = 3 * t + s0
             a1 = psa.tile([P, NPIX], F32, name="a1")
             for pi in range(4):
                 cols = slice(pi * P, (pi + 1) * P)
@@ -250,6 +278,12 @@ def tile_hyperpatchinvertedresidual_kernel(
                     rhs=xc[b][:, cols].bitcast(FP8X4), rhs_scale=xs[b][:, cols],
                     start=True, stop=True,
                 )
+            a1_t[i] = a1
+
+        def ev_a(i):
+            b, s0, t = a_order[i]
+            j = 3 * t + s0
+            a1 = a1_t[i]
             hp = hpool.tile([P, H + 2, WD + 2], F32, name="hp")
             inner = hp[:, 1 : H + 1, 1 : WD + 1]
             nc.scalar.activation(
@@ -274,78 +308,157 @@ def tile_hyperpatchinvertedresidual_kernel(
         h2c = [const.tile([P, 3, NPIX], U32, name="h2c%d" % b, align_bytes=64) for b in range(B)]
         h2s = [const.tile([P, 3, NPIX], U8, name="h2s%d" % b, align_bytes=64) for b in range(B)]
 
-        def depthwise(i):
+        def stt(i, pi, tap):
             b, s0, t = a_order[i]
-            j = 3 * t + s0
-            hp, acc = hp_t[i], acc_t[(b, s0)]
-            for tap in range(1, 9):
-                for pi in range(4):
-                    k = tap * 4 + fg_of(pi)
-                    nc.vector.scalar_tensor_tensor(
-                        out=accv(acc, t, pi), in0=win(hp, pi, tap // 3, tap % 3),
-                        scalar=k2f[b][:, j, k : k + 1], in1=accv(acc, t, pi),
-                        op0=ALU.mult, op1=ALU.add,
-                    )
-            if t == 3:
-                h2g = hgpool.tile([P, NPIX, 4], BF16, name="h2g", align_bytes=64)
-                nc.vector.tensor_scalar(
-                    out=h2g[:], in0=acc[:].rearrange("p t n -> p n t"),
-                    scalar1=0.0, scalar2=6.0, op0=ALU.max, op1=ALU.min,
-                )
-                nc.vector.quantize_mx(
-                    out=h2c[b][:, s0, :].bitcast(FP8X4), scales=h2s[b][:, s0, :],
-                    in_=h2g[:].rearrange("p n t -> p (n t)"),
-                )
+            k = tap * 4 + fg_of(pi)
+            acc = acc_t[(b, s0)]
+            nc.vector.scalar_tensor_tensor(
+                out=accv(acc, t, pi), in0=win(hp_t[i], pi, tap // 3, tap % 3),
+                scalar=k2f[b][:, 3 * t + s0, k : k + 1], in1=accv(acc, t, pi),
+                op0=ALU.mult, op1=ALU.add,
+            )
 
-        def step3(b):
-            for ct in range(NCT):
-                e3 = pse.tile([P, NPIX], F32, name="e3")
+        def dw(i, taps):
+            for tap in taps:
                 for pi in range(4):
-                    cols = slice(pi * P, (pi + 1) * P)
-                    for s0 in range(3):
-                        u = ct * 3 + s0
-                        nc.tensor.matmul_mx(
-                            out=e3[:, cols],
-                            lhsT=w3c[b][:, u, cols].bitcast(FP8X4), lhsT_scale=w3s[b][:, u, cols],
-                            rhs=h2c[b][:, s0, cols].bitcast(FP8X4), rhs_scale=h2s[b][:, s0, cols],
-                            start=(s0 == 0), stop=(s0 == 2),
-                        )
-                ot = opool.tile([P, NPIX], F32, name="ot")
-                for g_ in range(2):
-                    nc.vector.scalar_tensor_tensor(
-                        out=ot[:].rearrange("p (y g z) -> p g y z", y=H, g=2)[:, g_],
-                        in0=e3[:, g_ * 256 : (g_ + 1) * 256].rearrange("p (y z) -> p y z", y=H),
-                        scalar=inv[:, 24 + ct : 25 + ct],
-                        in1=xb[b][:, ct, :].rearrange("p (y g z) -> p g y z", y=H, g=2)[:, g_],
-                        op0=ALU.mult, op1=ALU.add,
-                    )
-                nc.sync.dma_start(
-                    out=out[b, ct * P : (ct + 1) * P].rearrange("c y z -> c (y z)"), in_=ot[:]
-                )
+                    stt(i, pi, tap)
 
-        n_a = len(a_order)
-        prep_x(0)
-        prep_a(0)
-        prep_bn()
+        def clip_q(b, s0, lo, n):
+            acc = acc_t[(b, s0)]
+            h2g = hgpool.tile([P, n, 4], BF16, name="h2g", align_bytes=64)
+            nc.vector.tensor_scalar(
+                out=h2g[:], in0=acc[:, :, lo : lo + n].rearrange("p t n -> p n t"),
+                scalar1=0.0, scalar2=6.0, op0=ALU.max, op1=ALU.min,
+            )
+            nc.vector.quantize_mx(
+                out=h2c[b][:, s0, lo : lo + n].bitcast(FP8X4), scales=h2s[b][:, s0, lo : lo + n],
+                in_=h2g[:].rearrange("p n t -> p (n t)"),
+            )
+
+        ot = [const.tile([P, NCT, NPIX], F32, name="ot%d" % b) for b in range(B)]
+        e3_t = {}
+
+        def mm_e(b, ct, pis):
+            e3 = e3_t[(b, ct)]
+            for pi in pis:
+                cols = slice(pi * P, (pi + 1) * P)
+                for s0 in range(3):
+                    u = ct * 3 + s0
+                    nc.tensor.matmul_mx(
+                        out=e3[:, cols],
+                        lhsT=w3c[b][:, u, cols].bitcast(FP8X4), lhsT_scale=w3s[b][:, u, cols],
+                        rhs=h2c[b][:, s0, cols].bitcast(FP8X4), rhs_scale=h2s[b][:, s0, cols],
+                        start=(s0 == 0), stop=(s0 == 2),
+                    )
+
+        def fin_half(b, ct, g_):
+            nc.vector.scalar_tensor_tensor(
+                out=ot[b][:, ct, :].rearrange("p (y g z) -> p g y z", y=H, g=2)[:, g_],
+                in0=e3_t[(b, ct)][:, g_ * 256 : (g_ + 1) * 256].rearrange("p (y z) -> p y z", y=H),
+                scalar=inv3[:, ct : ct + 1],
+                in1=xb[b][:, ct, :].rearrange("p (y g z) -> p g y z", y=H, g=2)[:, g_],
+                op0=ALU.mult, op1=ALU.add,
+            )
+
+        def fin_patch(b, ct, pi):
+            g_, f_ = pi // 2, pi % 2
+
+            def img(tl):
+                return tl[:, ct, :].rearrange("p (y z) -> p y z", y=H)[
+                    :, 8 * f_ : 8 * f_ + 8, 16 * g_ : 16 * g_ + 16
+                ]
+
+            nc.vector.scalar_tensor_tensor(
+                out=img(ot[b]),
+                in0=e3_t[(b, ct)][:, pi * P : (pi + 1) * P].rearrange("p (y z) -> p y z", y=8),
+                scalar=inv3[:, ct : ct + 1], in1=img(xb[b]),
+                op0=ALU.mult, op1=ALU.add,
+            )
+
+        t_a(0, vector_half=True)
+        regroup_x(0, "vs")
+        q_a(0)
+        q_x(0)
+        bn_first("a", praw, 24)
+        bn_second("a", 24, inv, beta)
+        nc.vector.tensor_scalar_mul(out=ninv2[:], in0=inv[:, 12:24], scalar1=-1.0)
         prep_k2(0)
-        front(0)
-        prep_a(1)
-        for i in range(n_a):
-            if i + 3 < n_a:
-                load_w1(i + 3)
-            if i + 2 < n_a:
-                prep_a(i + 2)
-            if i + 1 < n_a:
-                front(i + 1)
-            prep_c(i)
+        mm_a(0)
+        ev_a(0)
+        t_a(1)
+
+        c_at = {}
+        nxt = 0
+        for i in range(n_a - 2):
+            c_at[i] = [nxt]
+            nxt += 1
+            if i in (6, 16):
+                c_at[i].append(nxt)
+                nxt += 1
+
+        for i in range(n_a - 2):
+            b, s0, t = a_order[i]
+            if i + 4 < n_a:
+                ld_a(i + 4)
             if i == 2:
-                prep_xb(0)
+                bn_first("c", praw3, NCT)
+            if i + 2 < n_a:
+                t_a(i + 2)
+            if i == 0:
+                dw(0, range(1, 3))
+                q_a(1)
+            mm_a(i + 1)
+            ev_a(i + 1)
+            for c in c_at[i]:
+                t_c(c)
+            if 3 <= i < 3 + NCT:
+                prep_xb(0, i - 3)
             if i == 6:
-                prep_x(1)
+                regroup_x(1, "ss")
+            if 17 <= i < 17 + NCT:
+                prep_xb(1, i - 17)
+            dw(i, range(3, 5) if i == 0 else range(1, 5))
+            if i + 2 < n_a:
+                q_a(i + 2)
+            if i == n_a - 3:
+                mm_a(i + 2)
+                ev_a(i + 2)
+            dw(i, range(5, 9))
+            for c in c_at[i]:
+                q_c(c)
+            if i == 2:
+                bn_second("c", NCT, inv3, beta3)
+            if i == 7:
+                q_x(1)
                 prep_k2(1)
-            if i == 14:
-                prep_xb(1)
-            depthwise(i)
-            if i == 11:
-                step3(0)
-        step3(1)
+            if t == 3:
+                clip_q(b, s0, 0, NPIX)
+            if 13 <= i < 13 + NCT:
+                ct = i - 13
+                e3_t[(0, ct)] = pse.tile([P, NPIX], F32, name="e3")
+                mm_e(0, ct, range(4))
+            if 14 <= i < 14 + NCT:
+                fin_half(0, i - 14, 0)
+                fin_half(0, i - 14, 1)
+            if i == 19:
+                nc.sync.dma_start(out=outv[0], in_=ot[0][:])
+
+        for ct in range(NCT):
+            pool = pse if ct < 2 else psa
+            e3_t[(1, ct)] = pool.tile([P, NPIX], F32, name="e3" if ct < 2 else "a1")
+        order = [0, 2, 1, 3]
+        for n, pi in enumerate(order):
+            for tap in range(1, 9):
+                stt(n_a - 2, pi, tap)
+                stt(n_a - 1, pi, tap)
+            if n > 0:
+                for ct in range(NCT):
+                    fin_patch(1, ct, order[n - 1])
+            if n == 2:
+                nc.sync.dma_start(out=outv[1][:, :, 0:256], in_=ot[1][:, :, 0:256])
+            clip_q(1, 2, pi * P, P)
+            for ct in range(NCT):
+                mm_e(1, ct, [pi])
+        for ct in range(NCT):
+            fin_patch(1, ct, order[3])
+        nc.sync.dma_start(out=outv[1][:, :, 256:512], in_=ot[1][:, :, 256:512])

@@ -21,6 +21,8 @@ EPS = 1e-5
 NJ = HID // P
 NCT = C // P
 FLOPS = 2 * B * NPIX * (2 * HID * C + 9 * HID)
+S_TAPS = (1, 2, 3)
+V_TAPS = (4, 5, 6, 7, 8)
 
 
 def tile_hyperpatchinvertedresidual_kernel(
@@ -28,15 +30,17 @@ def tile_hyperpatchinvertedresidual_kernel(
 ):
     nc = tc.nc
     with ExitStack() as ctx:
-        ctx.enter_context(tc.manual_schedule())
         const = ctx.enter_context(tc.tile_pool(name="const", bufs=1))
-        raw1 = ctx.enter_context(tc.tile_pool(name="raw1", bufs=5))
+        raw1 = ctx.enter_context(tc.tile_pool(name="raw1", bufs=4))
         raw3 = ctx.enter_context(tc.tile_pool(name="raw3", bufs=2))
         grp = ctx.enter_context(tc.tile_pool(name="grp", bufs=4))
         w1q = ctx.enter_context(tc.tile_pool(name="w1q", bufs=3))
         hpool = ctx.enter_context(tc.tile_pool(name="hpool", bufs=4))
         apool = ctx.enter_context(tc.tile_pool(name="apool", bufs=2))
         hgpool = ctx.enter_context(tc.tile_pool(name="hgpool", bufs=2))
+        ppool = ctx.enter_context(tc.tile_pool(name="ppool", bufs=3))
+        xbpool = ctx.enter_context(tc.tile_pool(name="xbpool", bufs=1))
+        opool = ctx.enter_context(tc.tile_pool(name="opool", bufs=1))
         pst = ctx.enter_context(tc.psum_pool(name="pst", bufs=3))
         psa = ctx.enter_context(tc.psum_pool(name="psa", bufs=2))
         pse = ctx.enter_context(tc.psum_pool(name="pse", bufs=2))
@@ -100,15 +104,15 @@ def tile_hyperpatchinvertedresidual_kernel(
         ld_vec(nc.scalar, praw, b1, 24, NJ)
         ld_vec(nc.scalar, praw, g2, 12, NJ)
         ld_vec(nc.scalar, praw, v2, 84, NJ)
-        ld_vec(nc.gpsimd, praw, m2, 60, NJ)
-        ld_vec(nc.gpsimd, praw, b2, 36, NJ)
-        nc.gpsimd.dma_start(out=k2raw[0][:], in_=k2v[0])
         identf = const.tile([P, P], F32, name="identf")
         make_identity(nc, identf[:])
         ident = const.tile([P, P], BF16, name="ident")
         make_identity(nc, ident[:])
         ld_a(1)
         ld_x(1)
+        ld_vec(nc.scalar, praw, m2, 60, NJ)
+        ld_vec(nc.scalar, praw, b2, 36, NJ)
+        nc.scalar.dma_start(out=k2raw[0][:], in_=k2v[0])
         ld_a(2)
         ld_c(0)
         ld_a(3)
@@ -149,7 +153,7 @@ def tile_hyperpatchinvertedresidual_kernel(
 
         xc = [const.tile([P, NPIX], U32, name="xc%d" % b, align_bytes=64) for b in range(B)]
         xs = [const.tile([P, NPIX], U8, name="xs%d" % b, align_bytes=64) for b in range(B)]
-        xb = [const.tile([P, NCT, NPIX], F32, name="xb%d" % b) for b in range(B)]
+        xb = {}
         xg_t = {}
 
         def regroup_x(b, engs):
@@ -167,6 +171,8 @@ def tile_hyperpatchinvertedresidual_kernel(
             nc.vector.quantize_mx(out=xc[b][:].bitcast(FP8X4), scales=xs[b][:], in_=xg_t[b][:])
 
         def prep_xb(b, ct):
+            if ct == 0:
+                xb[b] = xbpool.tile([P, NCT, NPIX], F32, name="xb")
             nc.scalar.activation(
                 out=xb[b][:, ct, :], in_=xraw[b][:, ct, :], func=ACT.Identity,
                 bias=beta3[:, ct : ct + 1], scale=1.0,
@@ -257,6 +263,7 @@ def tile_hyperpatchinvertedresidual_kernel(
             )
 
         a1_t = {}
+        pb_t = {}
         hp_t = {}
         acc_t = {}
 
@@ -303,7 +310,17 @@ def tile_hyperpatchinvertedresidual_kernel(
                     out=accv(acc, t, pi), in_=win(hp, pi, 0, 0), func=ACT.Identity,
                     bias=bias2[b][:, j, fg : fg + 1], scale=k2f[b][:, j, fg : fg + 1],
                 )
+            pb = ppool.tile([P, len(S_TAPS), NPIX], F32, name="pb")
+            for n, tap in enumerate(S_TAPS):
+                for pi in range(4):
+                    k = tap * 4 + fg_of(pi)
+                    nc.scalar.activation(
+                        out=pb[:, n, pi * P : (pi + 1) * P].rearrange("p (y z) -> p y z", y=8),
+                        in_=win(hp, pi, tap // 3, tap % 3), func=ACT.Copy,
+                        scale=k2f[b][:, j, k : k + 1],
+                    )
             hp_t[i] = hp
+            pb_t[i] = pb
 
         h2c = [const.tile([P, 3, NPIX], U32, name="h2c%d" % b, align_bytes=64) for b in range(B)]
         h2s = [const.tile([P, 3, NPIX], U8, name="h2s%d" % b, align_bytes=64) for b in range(B)]
@@ -318,8 +335,18 @@ def tile_hyperpatchinvertedresidual_kernel(
                 op0=ALU.mult, op1=ALU.add,
             )
 
-        def dw(i, taps):
-            for tap in taps:
+        def add_products(i, lo, n):
+            b, s0, t = a_order[i]
+            acc = acc_t[(b, s0)]
+            for m in range(len(S_TAPS)):
+                nc.vector.tensor_tensor(
+                    out=acc[:, t, lo : lo + n], in0=acc[:, t, lo : lo + n],
+                    in1=pb_t[i][:, m, lo : lo + n], op=ALU.add,
+                )
+
+        def dw(i):
+            add_products(i, 0, NPIX)
+            for tap in V_TAPS:
                 for pi in range(4):
                     stt(i, pi, tap)
 
@@ -335,7 +362,7 @@ def tile_hyperpatchinvertedresidual_kernel(
                 in_=h2g[:].rearrange("p n t -> p (n t)"),
             )
 
-        ot = [const.tile([P, NCT, NPIX], F32, name="ot%d" % b) for b in range(B)]
+        ot = {}
         e3_t = {}
 
         def mm_e(b, ct, pis):
@@ -386,6 +413,7 @@ def tile_hyperpatchinvertedresidual_kernel(
         mm_a(0)
         ev_a(0)
         t_a(1)
+        q_a(1)
 
         c_at = {}
         nxt = 0
@@ -402,53 +430,47 @@ def tile_hyperpatchinvertedresidual_kernel(
                 ld_a(i + 4)
             if i == 2:
                 bn_first("c", praw3, NCT)
+                bn_second("c", NCT, inv3, beta3)
             if i + 2 < n_a:
                 t_a(i + 2)
-            if i == 0:
-                dw(0, range(1, 3))
-                q_a(1)
+                q_a(i + 2)
             mm_a(i + 1)
             ev_a(i + 1)
+            if i == n_a - 3:
+                mm_a(i + 2)
+                ev_a(i + 2)
             for c in c_at[i]:
                 t_c(c)
+                q_c(c)
             if 3 <= i < 3 + NCT:
                 prep_xb(0, i - 3)
             if i == 6:
                 regroup_x(1, "ss")
-            if 17 <= i < 17 + NCT:
-                prep_xb(1, i - 17)
-            dw(i, range(3, 5) if i == 0 else range(1, 5))
-            if i + 2 < n_a:
-                q_a(i + 2)
-            if i == n_a - 3:
-                mm_a(i + 2)
-                ev_a(i + 2)
-            dw(i, range(5, 9))
-            for c in c_at[i]:
-                q_c(c)
-            if i == 2:
-                bn_second("c", NCT, inv3, beta3)
-            if i == 7:
                 q_x(1)
                 prep_k2(1)
+            dw(i)
             if t == 3:
                 clip_q(b, s0, 0, NPIX)
-            if 13 <= i < 13 + NCT:
-                ct = i - 13
-                e3_t[(0, ct)] = pse.tile([P, NPIX], F32, name="e3")
-                mm_e(0, ct, range(4))
-            if 14 <= i < 14 + NCT:
-                fin_half(0, i - 14, 0)
-                fin_half(0, i - 14, 1)
-            if i == 19:
+            if i == 11:
+                ot[0] = opool.tile([P, NCT, NPIX], F32, name="ot")
+                for ct in range(NCT):
+                    e3_t[(0, ct)] = pse.tile([P, NPIX], F32, name="e3")
+                    mm_e(0, ct, range(4))
+                    fin_half(0, ct, 0)
+                    fin_half(0, ct, 1)
                 nc.sync.dma_start(out=outv[0], in_=ot[0][:])
+            if 13 <= i < 13 + NCT:
+                prep_xb(1, i - 13)
 
         for ct in range(NCT):
             pool = pse if ct < 2 else psa
             e3_t[(1, ct)] = pool.tile([P, NPIX], F32, name="e3" if ct < 2 else "a1")
+        ot[1] = opool.tile([P, NCT, NPIX], F32, name="ot")
         order = [0, 2, 1, 3]
         for n, pi in enumerate(order):
-            for tap in range(1, 9):
+            add_products(n_a - 2, pi * P, P)
+            add_products(n_a - 1, pi * P, P)
+            for tap in V_TAPS:
                 stt(n_a - 2, pi, tap)
                 stt(n_a - 1, pi, tap)
             if n > 0:

@@ -21,8 +21,6 @@ EPS = 1e-5
 NJ = HID // P
 NCT = C // P
 FLOPS = 2 * B * NPIX * (2 * HID * C + 9 * HID)
-S_TAPS = (1, 2, 3)
-V_TAPS = (4, 5, 6, 7, 8)
 
 
 def tile_hyperpatchinvertedresidual_kernel(
@@ -38,7 +36,6 @@ def tile_hyperpatchinvertedresidual_kernel(
         hpool = ctx.enter_context(tc.tile_pool(name="hpool", bufs=4))
         apool = ctx.enter_context(tc.tile_pool(name="apool", bufs=2))
         hgpool = ctx.enter_context(tc.tile_pool(name="hgpool", bufs=2))
-        ppool = ctx.enter_context(tc.tile_pool(name="ppool", bufs=3))
         xbpool = ctx.enter_context(tc.tile_pool(name="xbpool", bufs=1))
         opool = ctx.enter_context(tc.tile_pool(name="opool", bufs=1))
         pst = ctx.enter_context(tc.psum_pool(name="pst", bufs=3))
@@ -208,16 +205,6 @@ def tile_hyperpatchinvertedresidual_kernel(
         def t_a(i, vector_half=False):
             g = grp.tile([P, 2048], BF16, name="g", align_bytes=64)
             ga_t[i] = g
-            if i % 2 == 1:
-                t1 = t1_tiles[i]
-                for half in range(2):
-                    tp = pst.tile([P, 1024], BF16, name="tp")
-                    for kk in range(8):
-                        pi, a = 2 * half + kk // 4, kk % 4
-                        src = t1[:, a, :].rearrange("q (c e) -> q c e", e=4)[:, :, fg_of(pi)]
-                        nc.tensor.transpose(tp[:, kk * P : (kk + 1) * P], src, ident[:])
-                    nc.scalar.copy(out=g[:, half * 1024 : (half + 1) * 1024], in_=tp[:])
-                return
             t1w = t1_tiles[i][:].bitcast(F32)
             gv = g[:].rearrange("p (g f n) -> p f g n", g=2, f=2)
             for f_ in range(2):
@@ -263,7 +250,6 @@ def tile_hyperpatchinvertedresidual_kernel(
             )
 
         a1_t = {}
-        pb_t = {}
         hp_t = {}
         acc_t = {}
 
@@ -310,17 +296,7 @@ def tile_hyperpatchinvertedresidual_kernel(
                     out=accv(acc, t, pi), in_=win(hp, pi, 0, 0), func=ACT.Identity,
                     bias=bias2[b][:, j, fg : fg + 1], scale=k2f[b][:, j, fg : fg + 1],
                 )
-            pb = ppool.tile([P, len(S_TAPS), NPIX], F32, name="pb")
-            for n, tap in enumerate(S_TAPS):
-                for pi in range(4):
-                    k = tap * 4 + fg_of(pi)
-                    nc.scalar.activation(
-                        out=pb[:, n, pi * P : (pi + 1) * P].rearrange("p (y z) -> p y z", y=8),
-                        in_=win(hp, pi, tap // 3, tap % 3), func=ACT.Copy,
-                        scale=k2f[b][:, j, k : k + 1],
-                    )
             hp_t[i] = hp
-            pb_t[i] = pb
 
         h2c = [const.tile([P, 3, NPIX], U32, name="h2c%d" % b, align_bytes=64) for b in range(B)]
         h2s = [const.tile([P, 3, NPIX], U8, name="h2s%d" % b, align_bytes=64) for b in range(B)]
@@ -335,18 +311,8 @@ def tile_hyperpatchinvertedresidual_kernel(
                 op0=ALU.mult, op1=ALU.add,
             )
 
-        def add_products(i, lo, n):
-            b, s0, t = a_order[i]
-            acc = acc_t[(b, s0)]
-            for m in range(len(S_TAPS)):
-                nc.vector.tensor_tensor(
-                    out=acc[:, t, lo : lo + n], in0=acc[:, t, lo : lo + n],
-                    in1=pb_t[i][:, m, lo : lo + n], op=ALU.add,
-                )
-
         def dw(i):
-            add_products(i, 0, NPIX)
-            for tap in V_TAPS:
+            for tap in range(1, 9):
                 for pi in range(4):
                     stt(i, pi, tap)
 
@@ -468,9 +434,7 @@ def tile_hyperpatchinvertedresidual_kernel(
         ot[1] = opool.tile([P, NCT, NPIX], F32, name="ot")
         order = [0, 2, 1, 3]
         for n, pi in enumerate(order):
-            add_products(n_a - 2, pi * P, P)
-            add_products(n_a - 1, pi * P, P)
-            for tap in V_TAPS:
+            for tap in range(1, 9):
                 stt(n_a - 2, pi, tap)
                 stt(n_a - 1, pi, tap)
             if n > 0:

@@ -84,39 +84,39 @@ def tile_hyperpatchinvertedresidual_kernel(
 
         six = const.tile([P, 1], F32, name="six")
         nc.vector.memset(six[:], 6.0)
-        praw = const.tile([P, P], BF16, name="praw")
+        praw = const.tile([P, 3 * P], BF16, name="praw")
         nc.vector.memset(praw[:], 0.0)
         praw3 = const.tile([P, P], BF16, name="praw3")
         nc.vector.memset(praw3[:], 0.0)
 
-        def ld_vec(eng, dst, vec, r0, n):
-            eng.dma_start(out=dst[r0 : r0 + n, :], in_=vec.rearrange("(j e) -> j e", e=P))
+        def ld_vec(eng, dst, vec, r0):
+            eng.dma_start(out=dst[r0 : r0 + 4, :], in_=vec.rearrange("(r e) -> r e", r=4))
 
         k2raw = [const.tile([P, NJ, 36], BF16, name="k2raw%d" % b) for b in range(B)]
         ld_a(0)
         ld_x(0)
-        ld_vec(nc.scalar, praw, g1, 0, NJ)
-        ld_vec(nc.scalar, praw, v1, 72, NJ)
-        ld_vec(nc.scalar, praw, m1, 48, NJ)
-        ld_vec(nc.scalar, praw, b1, 24, NJ)
-        ld_vec(nc.scalar, praw, g2, 12, NJ)
-        ld_vec(nc.scalar, praw, v2, 84, NJ)
+        ld_vec(nc.scalar, praw, g1, 0)
+        ld_vec(nc.scalar, praw, v1, 24)
+        ld_vec(nc.scalar, praw, m1, 16)
+        ld_vec(nc.scalar, praw, b1, 8)
+        ld_vec(nc.scalar, praw, g2, 4)
+        ld_vec(nc.scalar, praw, v2, 28)
+        ld_vec(nc.scalar, praw, m2, 20)
+        ld_vec(nc.scalar, praw, b2, 12)
+        nc.scalar.dma_start(out=k2raw[0][:], in_=k2v[0])
         identf = const.tile([P, P], F32, name="identf")
         make_identity(nc, identf[:])
         ident = const.tile([P, P], BF16, name="ident")
         make_identity(nc, ident[:])
         ld_a(1)
-        ld_x(1)
-        ld_vec(nc.scalar, praw, m2, 60, NJ)
-        ld_vec(nc.scalar, praw, b2, 36, NJ)
-        nc.scalar.dma_start(out=k2raw[0][:], in_=k2v[0])
         ld_a(2)
-        ld_c(0)
         ld_a(3)
-        ld_vec(nc.sync, praw3, g3, 0, NCT)
-        ld_vec(nc.sync, praw3, v3, 12, NCT)
-        ld_vec(nc.sync, praw3, m3, 8, NCT)
-        ld_vec(nc.sync, praw3, b3, 4, NCT)
+        ld_c(0)
+        ld_x(1)
+        ld_vec(nc.sync, praw3, g3, 0)
+        ld_vec(nc.sync, praw3, v3, 12)
+        ld_vec(nc.sync, praw3, m3, 8)
+        ld_vec(nc.sync, praw3, b3, 4)
         nc.sync.dma_start(out=k2raw[1][:], in_=k2v[1])
         warm = const.tile([P, 1], F32, name="warm")
         nc.scalar.sqrt(out=warm[:], in_=six[:])
@@ -129,12 +129,20 @@ def tile_hyperpatchinvertedresidual_kernel(
         bn_tmp = {}
 
         def bn_first(key, src, n):
+            rows = 4 * n * P // src.shape[1]
+            blocks = src.shape[1] // P
             ptp = pst.tile([P, 1024], BF16, name="tp")
-            nc.tensor.transpose(ptp[:, 0:P], src[:], ident[:])
+            for s in range(blocks):
+                nc.tensor.transpose(
+                    ptp[:, s * P : (s + 1) * P], src[:, s * P : (s + 1) * P], ident[:]
+                )
             pf = const.tile([P, 4 * n], F32, name="pf" + key)
             ve = const.tile([P, n], F32, name="ve" + key)
             sd = const.tile([P, n], F32, name="sd" + key)
-            nc.vector.tensor_copy(out=pf[:], in_=ptp[:, 0 : 4 * n])
+            nc.vector.tensor_copy(
+                out=pf[:].rearrange("p (x s) -> p x s", s=blocks),
+                in_=ptp[:, 0 : blocks * P].rearrange("p (s x) -> p x s", s=blocks)[:, 0:rows, :],
+            )
             nc.vector.tensor_scalar_add(out=ve[:], in0=pf[:, 3 * n : 4 * n], scalar1=EPS)
             nc.scalar.sqrt(out=sd[:], in_=ve[:])
             bn_tmp[key] = (pf, sd)

@@ -20,6 +20,8 @@ N1, N2, N3 = HID * C, HID * 9, C * HID
 EPS = 1e-5
 NJ = HID // P
 NCT = C // P
+CENTRE = 4
+TAPS = [tap for tap in range(9) if tap != CENTRE]
 FLOPS = 2 * B * NPIX * (2 * HID * C + 9 * HID)
 
 
@@ -28,11 +30,15 @@ def tile_hyperpatchinvertedresidual_kernel(
 ):
     nc = tc.nc
     with ExitStack() as ctx:
+        ctx.enter_context(
+            tc.manual_schedule(engines={mybir.EngineType.SP, mybir.EngineType.Activation})
+        )
         const = ctx.enter_context(tc.tile_pool(name="const", bufs=1))
         raw1 = ctx.enter_context(tc.tile_pool(name="raw1", bufs=4))
         raw3 = ctx.enter_context(tc.tile_pool(name="raw3", bufs=2))
         grp = ctx.enter_context(tc.tile_pool(name="grp", bufs=4))
         w1q = ctx.enter_context(tc.tile_pool(name="w1q", bufs=3))
+        rpool = ctx.enter_context(tc.tile_pool(name="rpool", bufs=2))
         hpool = ctx.enter_context(tc.tile_pool(name="hpool", bufs=4))
         apool = ctx.enter_context(tc.tile_pool(name="apool", bufs=2))
         hgpool = ctx.enter_context(tc.tile_pool(name="hgpool", bufs=2))
@@ -99,11 +105,11 @@ def tile_hyperpatchinvertedresidual_kernel(
         ld_vec(nc.scalar, praw, v1, 24)
         ld_vec(nc.scalar, praw, m1, 16)
         ld_vec(nc.scalar, praw, b1, 8)
-        ld_vec(nc.scalar, praw, g2, 4)
-        ld_vec(nc.scalar, praw, v2, 28)
-        ld_vec(nc.scalar, praw, m2, 20)
-        ld_vec(nc.scalar, praw, b2, 12)
-        nc.scalar.dma_start(out=k2raw[0][:], in_=k2v[0])
+        nc.sync.dma_start(out=k2raw[0][:], in_=k2v[0])
+        ld_vec(nc.sync, praw, g2, 4)
+        ld_vec(nc.sync, praw, v2, 28)
+        ld_vec(nc.sync, praw, m2, 20)
+        ld_vec(nc.sync, praw, b2, 12)
         identf = const.tile([P, P], F32, name="identf")
         make_identity(nc, identf[:])
         ident = const.tile([P, P], BF16, name="ident")
@@ -210,20 +216,19 @@ def tile_hyperpatchinvertedresidual_kernel(
         w1c_t = {}
         w1s_t = {}
 
-        def t_a(i, vector_half=False):
-            g = grp.tile([P, 2048], BF16, name="g", align_bytes=64)
-            ga_t[i] = g
+        def t_a(i, f_, eng="s"):
+            if f_ == 0:
+                ga_t[i] = grp.tile([P, 2048], BF16, name="g", align_bytes=64)
             t1w = t1_tiles[i][:].bitcast(F32)
-            gv = g[:].rearrange("p (g f n) -> p f g n", g=2, f=2)
-            for f_ in range(2):
-                tp = pst.tile([P, 512], F32, name="tp")
-                for a in range(4):
-                    nc.tensor.transpose(tp[:, a * P : (a + 1) * P], t1w[:, a, f_:256:2], identf[:])
-                src = tp[:].bitcast(BF16).rearrange("p (n g) -> p g n", g=2)
-                if vector_half and f_ == 1:
-                    nc.vector.tensor_copy(out=gv[:, f_], in_=src)
-                else:
-                    nc.scalar.copy(out=gv[:, f_], in_=src)
+            dst = ga_t[i][:].rearrange("p (g f n) -> p f g n", g=2, f=2)[:, f_]
+            tp = pst.tile([P, 512], F32, name="tp")
+            for a in range(4):
+                nc.tensor.transpose(tp[:, a * P : (a + 1) * P], t1w[:, a, f_:256:2], identf[:])
+            src = tp[:].bitcast(BF16).rearrange("p (n g) -> p g n", g=2)
+            if eng == "v":
+                nc.vector.tensor_copy(out=dst, in_=src)
+            else:
+                nc.scalar.copy(out=dst, in_=src)
 
         def q_a(i):
             w1c = w1q.tile([P, 512], U32, name="w1c", align_bytes=64)
@@ -234,21 +239,20 @@ def tile_hyperpatchinvertedresidual_kernel(
         w3c = [const.tile([P, 12, 512], U32, name="w3c%d" % b, align_bytes=64) for b in range(B)]
         w3s = [const.tile([P, 12, 512], U8, name="w3s%d" % b, align_bytes=64) for b in range(B)]
 
-        def t_c(i):
+        def t_c(i, half):
             b, ct, s0 = c_order[i]
             k = b * NCT + ct
-            if s0 == 0 and k + 1 < B * NCT:
-                ld_c(k + 1)
+            if half == 0:
+                gc_t[i] = grp.tile([P, 2048], BF16, name="g", align_bytes=64)
+                if s0 == 0 and k + 1 < B * NCT:
+                    ld_c(k + 1)
             t3 = t3_tiles[k]
-            g = grp.tile([P, 2048], BF16, name="g", align_bytes=64)
-            for half in range(2):
-                tp = pst.tile([P, 1024], BF16, name="tp")
-                for kk in range(8):
-                    pi, a = 2 * half + kk // 4, kk % 4
-                    src = t3[:, a, :].rearrange("q (s o e) -> q s o e", s=3, e=4)[:, s0, :, fg_of(pi)]
-                    nc.tensor.transpose(tp[:, kk * P : (kk + 1) * P], src, ident[:])
-                nc.scalar.copy(out=g[:, half * 1024 : (half + 1) * 1024], in_=tp[:])
-            gc_t[i] = g
+            tp = pst.tile([P, 1024], BF16, name="tp")
+            for kk in range(8):
+                pi, a = 2 * half + kk // 4, kk % 4
+                src = t3[:, a, :].rearrange("q (s o e) -> q s o e", s=3, e=4)[:, s0, :, fg_of(pi)]
+                nc.tensor.transpose(tp[:, kk * P : (kk + 1) * P], src, ident[:])
+            nc.scalar.copy(out=gc_t[i][:, half * 1024 : (half + 1) * 1024], in_=tp[:])
 
         def q_c(i):
             b, ct, s0 = c_order[i]
@@ -281,30 +285,46 @@ def tile_hyperpatchinvertedresidual_kernel(
                 )
             a1_t[i] = a1
 
-        def ev_a(i):
+        r1_t = {}
+
+        def inner(i):
+            return hp_t[i][:, 1 : H + 1, 1 : WD + 1]
+
+        def ev_relu(i):
             b, s0, t = a_order[i]
             j = 3 * t + s0
-            a1 = a1_t[i]
-            hp = hpool.tile([P, H + 2, WD + 2], F32, name="hp")
-            inner = hp[:, 1 : H + 1, 1 : WD + 1]
+            r1_t[i] = rpool.tile([P, H, WD], F32, name="r1")
             nc.scalar.activation(
-                out=inner.rearrange("p y (g z) -> p g y z", g=2),
-                in_=a1[:].rearrange("p (g y z) -> p g y z", g=2, y=H),
+                out=r1_t[i][:].rearrange("p y (g z) -> p g y z", g=2),
+                in_=a1_t[i][:].rearrange("p (g y z) -> p g y z", g=2, y=H),
                 func=ACT.Relu, bias=beta[:, j : j + 1], scale=inv[:, j : j + 1],
             )
-            nc.scalar.activation(out=inner, in_=inner, func=ACT.Relu, bias=six[:], scale=-1.0)
+
+        def ev_clip(i):
+            hp_t[i] = hpool.tile([P, H + 2, WD + 2], F32, name="hp")
+            nc.scalar.activation(
+                out=inner(i), in_=r1_t[i][:], func=ACT.Relu, bias=six[:], scale=-1.0
+            )
+
+        def ev_columns(i):
+            hp = hp_t[i]
             nc.scalar.copy(out=hp[:, 1 : H + 1, 0 : WD + 2 : WD + 1], in_=hp[:, 1 : H + 1, 2:WD:29])
+
+        def ev_rows(i):
+            hp = hp_t[i]
             nc.scalar.copy(out=hp[:, 0 : H + 2 : H + 1, :], in_=hp[:, 2:H:13, :])
+
+        def ev_centre(i):
+            b, s0, t = a_order[i]
+            j = 3 * t + s0
             if t == 0:
                 acc_t[(b, s0)] = apool.tile([P, 4, NPIX], F32, name="acc")
-            acc = acc_t[(b, s0)]
             for pi in range(4):
-                fg = fg_of(pi)
+                k = 4 * CENTRE + fg_of(pi)
                 nc.scalar.activation(
-                    out=accv(acc, t, pi), in_=win(hp, pi, 0, 0), func=ACT.Identity,
-                    bias=bias2[b][:, j, fg : fg + 1], scale=k2f[b][:, j, fg : fg + 1],
+                    out=accv(acc_t[(b, s0)], t, pi), in_=win(hp_t[i], pi, 1, 1), func=ACT.Identity,
+                    bias=bias2[b][:, j, fg_of(pi) : fg_of(pi) + 1], scale=k2f[b][:, j, k : k + 1],
                 )
-            hp_t[i] = hp
 
         h2c = [const.tile([P, 3, NPIX], U32, name="h2c%d" % b, align_bytes=64) for b in range(B)]
         h2s = [const.tile([P, 3, NPIX], U8, name="h2s%d" % b, align_bytes=64) for b in range(B)]
@@ -320,7 +340,7 @@ def tile_hyperpatchinvertedresidual_kernel(
             )
 
         def dw(i):
-            for tap in range(1, 9):
+            for tap in TAPS:
                 for pi in range(4):
                     stt(i, pi, tap)
 
@@ -376,18 +396,28 @@ def tile_hyperpatchinvertedresidual_kernel(
                 op0=ALU.mult, op1=ALU.add,
             )
 
-        t_a(0, vector_half=True)
-        regroup_x(0, "vs")
-        q_a(0)
-        q_x(0)
-        bn_first("a", praw, 24)
-        bn_second("a", 24, inv, beta)
-        nc.vector.tensor_scalar_mul(out=ninv2[:], in0=inv[:, 12:24], scalar1=-1.0)
-        prep_k2(0)
-        mm_a(0)
-        ev_a(0)
-        t_a(1)
-        q_a(1)
+        def ev_a(i):
+            ev_relu(i)
+            ev_clip(i)
+            ev_columns(i)
+            ev_centre(i)
+            ev_rows(i)
+
+        with tc.manual_schedule():
+            t_a(0, 0, "s")
+            t_a(0, 1, "v")
+            regroup_x(0, "vs")
+            q_a(0)
+            q_x(0)
+            bn_first("a", praw, 24)
+            t_a(1, 0, "v")
+            bn_second("a", 24, inv, beta)
+            nc.vector.tensor_scalar_mul(out=ninv2[:], in0=inv[:, 12:24], scalar1=-1.0)
+            prep_k2(0)
+            mm_a(0)
+            t_a(1, 1, "v")
+            q_a(1)
+            ev_a(0)
 
         c_at = {}
         nxt = 0
@@ -405,16 +435,23 @@ def tile_hyperpatchinvertedresidual_kernel(
             if i == 2:
                 bn_first("c", praw3, NCT)
                 bn_second("c", NCT, inv3, beta3)
-            if i + 2 < n_a:
-                t_a(i + 2)
-                q_a(i + 2)
             mm_a(i + 1)
-            ev_a(i + 1)
+            ev_relu(i + 1)
+            if i + 2 < n_a:
+                t_a(i + 2, 0)
+            ev_clip(i + 1)
+            if i + 2 < n_a:
+                t_a(i + 2, 1)
+                q_a(i + 2)
+            ev_columns(i + 1)
+            ev_centre(i + 1)
+            ev_rows(i + 1)
             if i == n_a - 3:
                 mm_a(i + 2)
                 ev_a(i + 2)
             for c in c_at[i]:
-                t_c(c)
+                t_c(c, 0)
+                t_c(c, 1)
                 q_c(c)
             if 3 <= i < 3 + NCT:
                 prep_xb(0, i - 3)
@@ -442,7 +479,7 @@ def tile_hyperpatchinvertedresidual_kernel(
         ot[1] = opool.tile([P, NCT, NPIX], F32, name="ot")
         order = [0, 2, 1, 3]
         for n, pi in enumerate(order):
-            for tap in range(1, 9):
+            for tap in TAPS:
                 stt(n_a - 2, pi, tap)
                 stt(n_a - 1, pi, tap)
             if n > 0:

@@ -21,7 +21,7 @@ EPS = 1e-5
 NJ = HID // P
 NCT = C // P
 CENTRE = 4
-TAPS = [tap for tap in range(9) if tap != CENTRE]
+TAPS = [3, 5, 0, 1, 2, 6, 7, 8]
 FLOPS = 2 * B * NPIX * (2 * HID * C + 9 * HID)
 
 
@@ -410,14 +410,18 @@ def tile_hyperpatchinvertedresidual_kernel(
             q_a(0)
             q_x(0)
             bn_first("a", praw, 24)
-            t_a(1, 0, "v")
+            t_a(1, 0)
             bn_second("a", 24, inv, beta)
             nc.vector.tensor_scalar_mul(out=ninv2[:], in0=inv[:, 12:24], scalar1=-1.0)
             prep_k2(0)
             mm_a(0)
-            t_a(1, 1, "v")
+            ev_relu(0)
+            t_a(1, 1)
             q_a(1)
-            ev_a(0)
+            ev_clip(0)
+            ev_columns(0)
+            ev_centre(0)
+            ev_rows(0)
 
         c_at = {}
         nxt = 0
@@ -477,19 +481,19 @@ def tile_hyperpatchinvertedresidual_kernel(
             pool = pse if ct < 2 else psa
             e3_t[(1, ct)] = pool.tile([P, NPIX], F32, name="e3" if ct < 2 else "a1")
         ot[1] = opool.tile([P, NCT, NPIX], F32, name="ot")
-        order = [0, 2, 1, 3]
-        for n, pi in enumerate(order):
+        for f_ in range(2):
+            pis = [f_, 2 + f_]
             for tap in TAPS:
-                stt(n_a - 2, pi, tap)
-                stt(n_a - 1, pi, tap)
-            if n > 0:
+                for pi in pis:
+                    stt(n_a - 2, pi, tap)
+                    stt(n_a - 1, pi, tap)
+            for pi in pis:
+                clip_q(1, 2, pi * P, P)
                 for ct in range(NCT):
-                    fin_patch(1, ct, order[n - 1])
-            if n == 2:
-                nc.sync.dma_start(out=outv[1][:, :, 0:256], in_=ot[1][:, :, 0:256])
-            clip_q(1, 2, pi * P, P)
+                    mm_e(1, ct, [pi])
+        for f_ in range(2):
             for ct in range(NCT):
-                mm_e(1, ct, [pi])
-        for ct in range(NCT):
-            fin_patch(1, ct, order[3])
-        nc.sync.dma_start(out=outv[1][:, :, 256:512], in_=ot[1][:, :, 256:512])
+                for pi in (f_, 2 + f_):
+                    fin_patch(1, ct, pi)
+            rows = slice(f_ * 256, (f_ + 1) * 256)
+            nc.sync.dma_start(out=outv[1][:, :, rows], in_=ot[1][:, :, rows])

@@ -20,6 +20,7 @@ N1, N2, N3 = HID * C, HID * 9, C * HID
 EPS = 1e-5
 NJ = HID // P
 NCT = C // P
+PE_PATCH = 3
 CENTRE = 4
 TAPS = [3, 5, 0, 1, 2, 6, 7, 8]
 FLOPS = 2 * B * NPIX * (2 * HID * C + 9 * HID)
@@ -31,13 +32,14 @@ def tile_hyperpatchinvertedresidual_kernel(
     nc = tc.nc
     with ExitStack() as ctx:
         ctx.enter_context(
-            tc.manual_schedule(engines={mybir.EngineType.SP, mybir.EngineType.Activation})
+            tc.manual_schedule(engines={mybir.EngineType.SP, mybir.EngineType.Activation, mybir.EngineType.PE})
         )
         const = ctx.enter_context(tc.tile_pool(name="const", bufs=1))
         raw1 = ctx.enter_context(tc.tile_pool(name="raw1", bufs=4))
         raw3 = ctx.enter_context(tc.tile_pool(name="raw3", bufs=2))
         grp = ctx.enter_context(tc.tile_pool(name="grp", bufs=4))
         w1q = ctx.enter_context(tc.tile_pool(name="w1q", bufs=3))
+        dpool = ctx.enter_context(tc.tile_pool(name="dpool", bufs=2))
         rpool = ctx.enter_context(tc.tile_pool(name="rpool", bufs=2))
         hpool = ctx.enter_context(tc.tile_pool(name="hpool", bufs=4))
         apool = ctx.enter_context(tc.tile_pool(name="apool", bufs=2))
@@ -47,6 +49,7 @@ def tile_hyperpatchinvertedresidual_kernel(
         pst = ctx.enter_context(tc.psum_pool(name="pst", bufs=3))
         psa = ctx.enter_context(tc.psum_pool(name="psa", bufs=2))
         pse = ctx.enter_context(tc.psum_pool(name="pse", bufs=2))
+        psd = ctx.enter_context(tc.psum_pool(name="psd", bufs=1))
 
         w1v = [
             w[b, 0:N1].rearrange("(j a q c) f g -> q j a (c f g)", j=NJ, a=4, q=P)
@@ -319,7 +322,7 @@ def tile_hyperpatchinvertedresidual_kernel(
             j = 3 * t + s0
             if t == 0:
                 acc_t[(b, s0)] = apool.tile([P, 4, NPIX], F32, name="acc")
-            for pi in range(4):
+            for pi in vector_patches(i):
                 k = 4 * CENTRE + fg_of(pi)
                 nc.scalar.activation(
                     out=accv(acc_t[(b, s0)], t, pi), in_=win(hp_t[i], pi, 1, 1), func=ACT.Identity,
@@ -328,6 +331,40 @@ def tile_hyperpatchinvertedresidual_kernel(
 
         h2c = [const.tile([P, 3, NPIX], U32, name="h2c%d" % b, align_bytes=64) for b in range(B)]
         h2s = [const.tile([P, 3, NPIX], U8, name="h2s%d" % b, align_bytes=64) for b in range(B)]
+
+        def vector_patches(i):
+            return [pi for pi in range(4) if not (i % 4 == 0 and pi == PE_PATCH)]
+
+        dg_t = {}
+        d_t = {}
+
+        def make_dg(i, taps):
+            b, s0, t = a_order[i]
+            if taps[0] == 0:
+                dg_t[i] = dpool.tile([P, 9, P], F32, name="dg")
+            for tap in taps:
+                k = 4 * tap + fg_of(PE_PATCH)
+                nc.scalar.activation(
+                    out=dg_t[i][:, tap, :], in_=identf[:], func=ACT.Copy,
+                    scale=k2f[b][:, 3 * t + s0, k : k + 1],
+                )
+
+        def mm_d(i, tap):
+            if tap == 0:
+                d_t[i] = psd.tile([P, NPIX], F32, name="d")
+            nc.tensor.matmul(
+                d_t[i][:, 0:P].rearrange("p (y z) -> p y z", y=8),
+                lhsT=dg_t[i][:, tap, :], rhs=win(hp_t[i], PE_PATCH, tap // 3, tap % 3),
+                start=(tap == 0), stop=(tap == 8),
+            )
+
+        def ev_d(i):
+            b, s0, t = a_order[i]
+            fg = fg_of(PE_PATCH)
+            nc.scalar.activation(
+                out=acc_t[(b, s0)][:, t, PE_PATCH * P : (PE_PATCH + 1) * P], in_=d_t[i][:, 0:P],
+                func=ACT.Identity, bias=bias2[b][:, 3 * t + s0, fg : fg + 1], scale=1.0,
+            )
 
         def stt(i, pi, tap):
             b, s0, t = a_order[i]
@@ -341,7 +378,7 @@ def tile_hyperpatchinvertedresidual_kernel(
 
         def dw(i):
             for tap in TAPS:
-                for pi in range(4):
+                for pi in vector_patches(i):
                     stt(i, pi, tap)
 
         def clip_q(b, s0, lo, n):
@@ -439,14 +476,31 @@ def tile_hyperpatchinvertedresidual_kernel(
             if i == 2:
                 bn_first("c", praw3, NCT)
                 bn_second("c", NCT, inv3, beta3)
+            pe_tile, pe_step = i - i % 4, i % 4
+            pe_taps = [3 * pe_step + n for n in range(3)] if pe_step < 3 else []
             mm_a(i + 1)
+            if 13 <= i < 13 + NCT:
+                if i == 13:
+                    ot[0] = opool.tile([P, NCT, NPIX], F32, name="ot")
+                e3_t[(0, i - 13)] = pse.tile([P, NPIX], F32, name="e3")
+                mm_e(0, i - 13, range(4))
             ev_relu(i + 1)
+            if pe_step == 3:
+                ev_d(pe_tile)
             if i + 2 < n_a:
                 t_a(i + 2, 0)
             ev_clip(i + 1)
+            if i == 0:
+                make_dg(0, [0, 1, 2])
             if i + 2 < n_a:
                 t_a(i + 2, 1)
                 q_a(i + 2)
+            for tap in pe_taps[0:1]:
+                mm_d(pe_tile, tap)
+            if pe_step < 2:
+                make_dg(pe_tile, [3 * pe_step + 3 + n for n in range(3)])
+            if pe_step == 3 and i + 1 < n_a:
+                make_dg(i + 1, [0, 1, 2])
             ev_columns(i + 1)
             ev_centre(i + 1)
             ev_rows(i + 1)
@@ -455,8 +509,13 @@ def tile_hyperpatchinvertedresidual_kernel(
                 ev_a(i + 2)
             for c in c_at[i]:
                 t_c(c, 0)
+                if c == c_at[i][0]:
+                    for tap in pe_taps[1:2]:
+                        mm_d(pe_tile, tap)
                 t_c(c, 1)
                 q_c(c)
+            for tap in pe_taps[2:3]:
+                mm_d(pe_tile, tap)
             if 3 <= i < 3 + NCT:
                 prep_xb(0, i - 3)
             if i == 6:
@@ -466,16 +525,17 @@ def tile_hyperpatchinvertedresidual_kernel(
             dw(i)
             if t == 3:
                 clip_q(b, s0, 0, NPIX)
-            if i == 11:
-                ot[0] = opool.tile([P, NCT, NPIX], F32, name="ot")
-                for ct in range(NCT):
-                    e3_t[(0, ct)] = pse.tile([P, NPIX], F32, name="e3")
-                    mm_e(0, ct, range(4))
-                    fin_half(0, ct, 0)
-                    fin_half(0, ct, 1)
-                nc.sync.dma_start(out=outv[0], in_=ot[0][:])
             if 13 <= i < 13 + NCT:
-                prep_xb(1, i - 13)
+                fin_half(0, i - 13, 0)
+                fin_half(0, i - 13, 1)
+            if i == 13 + NCT:
+                nc.sync.dma_start(out=outv[0], in_=ot[0][:])
+            if 17 <= i < 17 + NCT:
+                prep_xb(1, i - 17)
+
+        for tap in (6, 7, 8):
+            mm_d(n_a - 4, tap)
+        ev_d(n_a - 4)
 
         for ct in range(NCT):
             pool = pse if ct < 2 else psa

@@ -21,6 +21,7 @@ EPS = 1e-5
 NJ = HID // P
 NCT = C // P
 PE_PATCH = 3
+PE_FIRST = 4
 CENTRE = 4
 TAPS = [3, 5, 0, 1, 2, 6, 7, 8]
 FLOPS = 2 * B * NPIX * (2 * HID * C + 9 * HID)
@@ -31,14 +32,12 @@ def tile_hyperpatchinvertedresidual_kernel(
 ):
     nc = tc.nc
     with ExitStack() as ctx:
-        ctx.enter_context(
-            tc.manual_schedule(engines={mybir.EngineType.SP, mybir.EngineType.Activation, mybir.EngineType.PE})
-        )
+        ctx.enter_context(tc.manual_schedule())
         const = ctx.enter_context(tc.tile_pool(name="const", bufs=1))
         raw1 = ctx.enter_context(tc.tile_pool(name="raw1", bufs=4))
         raw3 = ctx.enter_context(tc.tile_pool(name="raw3", bufs=2))
-        grp = ctx.enter_context(tc.tile_pool(name="grp", bufs=4))
-        w1q = ctx.enter_context(tc.tile_pool(name="w1q", bufs=3))
+        grp = ctx.enter_context(tc.tile_pool(name="grp", bufs=6))
+        w1q = ctx.enter_context(tc.tile_pool(name="w1q", bufs=4))
         dpool = ctx.enter_context(tc.tile_pool(name="dpool", bufs=2))
         rpool = ctx.enter_context(tc.tile_pool(name="rpool", bufs=2))
         hpool = ctx.enter_context(tc.tile_pool(name="hpool", bufs=4))
@@ -46,9 +45,9 @@ def tile_hyperpatchinvertedresidual_kernel(
         hgpool = ctx.enter_context(tc.tile_pool(name="hgpool", bufs=2))
         xbpool = ctx.enter_context(tc.tile_pool(name="xbpool", bufs=1))
         opool = ctx.enter_context(tc.tile_pool(name="opool", bufs=1))
-        pst = ctx.enter_context(tc.psum_pool(name="pst", bufs=3))
-        psa = ctx.enter_context(tc.psum_pool(name="psa", bufs=2))
-        pse = ctx.enter_context(tc.psum_pool(name="pse", bufs=2))
+        pst = ctx.enter_context(tc.psum_pool(name="pst", bufs=5))
+        psa = ctx.enter_context(tc.psum_pool(name="psa", bufs=1))
+        pse = ctx.enter_context(tc.psum_pool(name="pse", bufs=1))
         psd = ctx.enter_context(tc.psum_pool(name="psd", bufs=1))
 
         w1v = [
@@ -103,12 +102,11 @@ def tile_hyperpatchinvertedresidual_kernel(
 
         k2raw = [const.tile([P, NJ, 36], BF16, name="k2raw%d" % b) for b in range(B)]
         ld_a(0)
-        ld_x(0)
         ld_vec(nc.scalar, praw, g1, 0)
         ld_vec(nc.scalar, praw, v1, 24)
         ld_vec(nc.scalar, praw, m1, 16)
         ld_vec(nc.scalar, praw, b1, 8)
-        nc.sync.dma_start(out=k2raw[0][:], in_=k2v[0])
+        ld_x(0)
         ld_vec(nc.sync, praw, g2, 4)
         ld_vec(nc.sync, praw, v2, 28)
         ld_vec(nc.sync, praw, m2, 20)
@@ -118,6 +116,7 @@ def tile_hyperpatchinvertedresidual_kernel(
         ident = const.tile([P, P], BF16, name="ident")
         make_identity(nc, ident[:])
         ld_a(1)
+        nc.sync.dma_start(out=k2raw[0][:], in_=k2v[0])
         ld_a(2)
         ld_a(3)
         ld_c(0)
@@ -137,10 +136,10 @@ def tile_hyperpatchinvertedresidual_kernel(
         ninv2 = const.tile([P, NJ], F32, name="ninv2")
         bn_tmp = {}
 
-        def bn_first(key, src, n):
+        def bn_first(key, src, n, pool, tag):
             rows = 4 * n * P // src.shape[1]
             blocks = src.shape[1] // P
-            ptp = pst.tile([P, 1024], BF16, name="tp")
+            ptp = pool.tile([P, 1024], BF16, name=tag)
             for s in range(blocks):
                 nc.tensor.transpose(
                     ptp[:, s * P : (s + 1) * P], src[:, s * P : (s + 1) * P], ident[:]
@@ -152,12 +151,15 @@ def tile_hyperpatchinvertedresidual_kernel(
                 out=pf[:].rearrange("p (x s) -> p x s", s=blocks),
                 in_=ptp[:, 0 : blocks * P].rearrange("p (s x) -> p x s", s=blocks)[:, 0:rows, :],
             )
+            bn_tmp[key] = (pf, ve, sd)
+
+        def bn_variance(key, n):
+            pf, ve, sd = bn_tmp[key]
             nc.vector.tensor_scalar_add(out=ve[:], in0=pf[:, 3 * n : 4 * n], scalar1=EPS)
             nc.scalar.sqrt(out=sd[:], in_=ve[:])
-            bn_tmp[key] = (pf, sd)
 
         def bn_second(key, n, inv_o, beta_o):
-            pf, sd = bn_tmp[key]
+            pf, ve, sd = bn_tmp[key]
             rsd = const.tile([P, n], F32, name="rsd" + key)
             mi = const.tile([P, n], F32, name="mi" + key)
             nc.vector.reciprocal(out=rsd[:], in_=sd[:])
@@ -219,19 +221,30 @@ def tile_hyperpatchinvertedresidual_kernel(
         w1c_t = {}
         w1s_t = {}
 
-        def t_a(i, f_, eng="s"):
+        tpa_t = {}
+
+        def transposes_a(i, f_):
+            t1w = t1_tiles[i][:].bitcast(F32)
+            tpa_t[f_] = pst.tile([P, 512], F32, name="tp")
+            for a in range(4):
+                nc.tensor.transpose(
+                    tpa_t[f_][:, a * P : (a + 1) * P], t1w[:, a, f_:256:2], identf[:]
+                )
+
+        def copy_a(i, f_, eng="s"):
             if f_ == 0:
                 ga_t[i] = grp.tile([P, 2048], BF16, name="g", align_bytes=64)
-            t1w = t1_tiles[i][:].bitcast(F32)
             dst = ga_t[i][:].rearrange("p (g f n) -> p f g n", g=2, f=2)[:, f_]
-            tp = pst.tile([P, 512], F32, name="tp")
-            for a in range(4):
-                nc.tensor.transpose(tp[:, a * P : (a + 1) * P], t1w[:, a, f_:256:2], identf[:])
+            tp = tpa_t[f_]
             src = tp[:].bitcast(BF16).rearrange("p (n g) -> p g n", g=2)
             if eng == "v":
                 nc.vector.tensor_copy(out=dst, in_=src)
             else:
                 nc.scalar.copy(out=dst, in_=src)
+
+        def t_a(i, f_, eng="s"):
+            transposes_a(i, f_)
+            copy_a(i, f_, eng)
 
         def q_a(i):
             w1c = w1q.tile([P, 512], U32, name="w1c", align_bytes=64)
@@ -242,20 +255,27 @@ def tile_hyperpatchinvertedresidual_kernel(
         w3c = [const.tile([P, 12, 512], U32, name="w3c%d" % b, align_bytes=64) for b in range(B)]
         w3s = [const.tile([P, 12, 512], U8, name="w3s%d" % b, align_bytes=64) for b in range(B)]
 
-        def t_c(i, half):
+        tpc_t = {}
+
+        def transposes_c(i, half):
             b, ct, s0 = c_order[i]
             k = b * NCT + ct
-            if half == 0:
-                gc_t[i] = grp.tile([P, 2048], BF16, name="g", align_bytes=64)
-                if s0 == 0 and k + 1 < B * NCT:
-                    ld_c(k + 1)
+            if half == 0 and s0 == 0 and k + 1 < B * NCT:
+                ld_c(k + 1)
             t3 = t3_tiles[k]
             tp = pst.tile([P, 1024], BF16, name="tp")
             for kk in range(8):
                 pi, a = 2 * half + kk // 4, kk % 4
                 src = t3[:, a, :].rearrange("q (s o e) -> q s o e", s=3, e=4)[:, s0, :, fg_of(pi)]
                 nc.tensor.transpose(tp[:, kk * P : (kk + 1) * P], src, ident[:])
-            nc.scalar.copy(out=gc_t[i][:, half * 1024 : (half + 1) * 1024], in_=tp[:])
+            tpc_t[(i, half)] = tp
+
+        def copy_c(i, half):
+            if half == 0:
+                gc_t[i] = grp.tile([P, 2048], BF16, name="g", align_bytes=64)
+            nc.scalar.copy(
+                out=gc_t[i][:, half * 1024 : (half + 1) * 1024], in_=tpc_t[(i, half)][:]
+            )
 
         def q_c(i):
             b, ct, s0 = c_order[i]
@@ -332,31 +352,33 @@ def tile_hyperpatchinvertedresidual_kernel(
         h2c = [const.tile([P, 3, NPIX], U32, name="h2c%d" % b, align_bytes=64) for b in range(B)]
         h2s = [const.tile([P, 3, NPIX], U8, name="h2s%d" % b, align_bytes=64) for b in range(B)]
 
+        def pe_tile(i):
+            return i >= n_a - 2 or (i >= PE_FIRST and (i - PE_FIRST) % 3 == 0 and i < n_a - 3)
+
         def vector_patches(i):
-            return [pi for pi in range(4) if not (i % 4 == 0 and pi == PE_PATCH)]
+            return [pi for pi in range(4) if not (pe_tile(i) and pi == PE_PATCH)]
 
         dg_t = {}
         d_t = {}
 
-        def make_dg(i, taps):
+        def make_dg(i):
             b, s0, t = a_order[i]
-            if taps[0] == 0:
-                dg_t[i] = dpool.tile([P, 9, P], F32, name="dg")
-            for tap in taps:
+            dg_t[i] = dpool.tile([P, 9, P], F32, name="dg")
+            for tap in range(9):
                 k = 4 * tap + fg_of(PE_PATCH)
                 nc.scalar.activation(
                     out=dg_t[i][:, tap, :], in_=identf[:], func=ACT.Copy,
                     scale=k2f[b][:, 3 * t + s0, k : k + 1],
                 )
 
-        def mm_d(i, tap):
-            if tap == 0:
-                d_t[i] = psd.tile([P, NPIX], F32, name="d")
-            nc.tensor.matmul(
-                d_t[i][:, 0:P].rearrange("p (y z) -> p y z", y=8),
-                lhsT=dg_t[i][:, tap, :], rhs=win(hp_t[i], PE_PATCH, tap // 3, tap % 3),
-                start=(tap == 0), stop=(tap == 8),
-            )
+        def mm_d(i):
+            d_t[i] = psd.tile([P, NPIX], F32, name="d")
+            for tap in range(9):
+                nc.tensor.matmul(
+                    d_t[i][:, 0:P].rearrange("p (y z) -> p y z", y=8),
+                    lhsT=dg_t[i][:, tap, :], rhs=win(hp_t[i], PE_PATCH, tap // 3, tap % 3),
+                    start=(tap == 0), stop=(tap == 8),
+                )
 
         def ev_d(i):
             b, s0, t = a_order[i]
@@ -376,18 +398,24 @@ def tile_hyperpatchinvertedresidual_kernel(
                 op0=ALU.mult, op1=ALU.add,
             )
 
-        def dw(i):
-            for tap in TAPS:
+        def dw(i, taps):
+            for tap in taps:
                 for pi in vector_patches(i):
                     stt(i, pi, tap)
 
-        def clip_q(b, s0, lo, n):
+        h2g_t = {}
+
+        def clip(b, s0, lo, n):
             acc = acc_t[(b, s0)]
             h2g = hgpool.tile([P, n, 4], BF16, name="h2g", align_bytes=64)
             nc.vector.tensor_scalar(
                 out=h2g[:], in0=acc[:, :, lo : lo + n].rearrange("p t n -> p n t"),
                 scalar1=0.0, scalar2=6.0, op0=ALU.max, op1=ALU.min,
             )
+            h2g_t[(b, s0, lo)] = h2g
+
+        def q_h(b, s0, lo, n):
+            h2g = h2g_t[(b, s0, lo)]
             nc.vector.quantize_mx(
                 out=h2c[b][:, s0, lo : lo + n].bitcast(FP8X4), scales=h2s[b][:, s0, lo : lo + n],
                 in_=h2g[:].rearrange("p n t -> p (n t)"),
@@ -433,127 +461,144 @@ def tile_hyperpatchinvertedresidual_kernel(
                 op0=ALU.mult, op1=ALU.add,
             )
 
-        def ev_a(i):
-            ev_relu(i)
-            ev_clip(i)
-            ev_columns(i)
-            ev_centre(i)
-            ev_rows(i)
+        t_a(0, 0, "s")
+        t_a(0, 1, "v")
+        regroup_x(0, "vs")
+        bn_first("a", praw, 24, pst, "tp")
+        t_a(1, 0)
+        q_a(0)
+        bn_variance("a", 24)
+        t_a(1, 1)
+        q_x(0)
+        bn_second("a", 24, inv, beta)
+        nc.vector.tensor_scalar_mul(out=ninv2[:], in0=inv[:, 12:24], scalar1=-1.0)
+        mm_a(0)
+        ev_relu(0)
+        prep_k2(0)
+        ev_clip(0)
+        ev_columns(0)
+        ev_centre(0)
+        ev_rows(0)
+        q_a(1)
 
-        with tc.manual_schedule():
-            t_a(0, 0, "s")
-            t_a(0, 1, "v")
-            regroup_x(0, "vs")
-            q_a(0)
-            q_x(0)
-            bn_first("a", praw, 24)
-            t_a(1, 0)
-            bn_second("a", 24, inv, beta)
-            nc.vector.tensor_scalar_mul(out=ninv2[:], in0=inv[:, 12:24], scalar1=-1.0)
-            prep_k2(0)
-            mm_a(0)
-            ev_relu(0)
-            t_a(1, 1)
-            q_a(1)
-            ev_clip(0)
-            ev_columns(0)
-            ev_centre(0)
-            ev_rows(0)
-
-        c_at = {}
+        c_at = {0: []}
         nxt = 0
-        for i in range(n_a - 2):
+        for i in range(1, n_a - 2):
             c_at[i] = [nxt]
             nxt += 1
-            if i in (6, 16):
+            if i in (6, 11, 16):
                 c_at[i].append(nxt)
                 nxt += 1
+        e_at = {14: 0, 15: 1, 17: 2, 18: 3}
+        h2_at = {}
+        c_late = []
 
         for i in range(n_a - 2):
             b, s0, t = a_order[i]
             if i + 4 < n_a:
                 ld_a(i + 4)
-            if i == 2:
-                bn_first("c", praw3, NCT)
-                bn_second("c", NCT, inv3, beta3)
-            pe_tile, pe_step = i - i % 4, i % 4
-            pe_taps = [3 * pe_step + n for n in range(3)] if pe_step < 3 else []
-            mm_a(i + 1)
-            if 13 <= i < 13 + NCT:
-                if i == 13:
-                    ot[0] = opool.tile([P, NCT, NPIX], F32, name="ot")
-                e3_t[(0, i - 13)] = pse.tile([P, NPIX], F32, name="e3")
-                mm_e(0, i - 13, range(4))
-            ev_relu(i + 1)
-            if pe_step == 3:
-                ev_d(pe_tile)
-            if i + 2 < n_a:
+            more = i + 2 < n_a
+            if more:
                 t_a(i + 2, 0)
+            dw(i, TAPS[0:1])
+            if i in h2_at:
+                q_h(*h2_at[i], 0, NPIX)
+            if more:
+                transposes_a(i + 2, 1)
+            mm_a(i + 1)
+            if i in e_at:
+                ct = e_at[i]
+                if ct == 0:
+                    ot[0] = opool.tile([P, NCT, NPIX], F32, name="ot")
+                e3_t[(0, ct)] = pse.tile([P, NPIX], F32, name="e3")
+                mm_e(0, ct, range(4))
+            if pe_tile(i):
+                mm_d(i)
+            ev_relu(i + 1)
+            if more:
+                copy_a(i + 2, 1)
             ev_clip(i + 1)
-            if i == 0:
-                make_dg(0, [0, 1, 2])
-            if i + 2 < n_a:
-                t_a(i + 2, 1)
-                q_a(i + 2)
-            for tap in pe_taps[0:1]:
-                mm_d(pe_tile, tap)
-            if pe_step < 2:
-                make_dg(pe_tile, [3 * pe_step + 3 + n for n in range(3)])
-            if pe_step == 3 and i + 1 < n_a:
-                make_dg(i + 1, [0, 1, 2])
             ev_columns(i + 1)
             ev_centre(i + 1)
             ev_rows(i + 1)
-            if i == n_a - 3:
-                mm_a(i + 2)
-                ev_a(i + 2)
-            for c in c_at[i]:
-                t_c(c, 0)
-                if c == c_at[i][0]:
-                    for tap in pe_taps[1:2]:
-                        mm_d(pe_tile, tap)
-                t_c(c, 1)
+            if i == 2:
+                bn_first("c", praw3, NCT, psd, "d")
+                bn_variance("c", NCT)
+            dw(i, TAPS[1:3])
+            if i == 3:
+                bn_second("c", NCT, inv3, beta3)
+            if more and i > 0:
+                q_a(i + 2)
+            dw(i, TAPS[3:5])
+            if i == 0:
+                q_a(2)
+            for c in c_late:
                 q_c(c)
-            for tap in pe_taps[2:3]:
-                mm_d(pe_tile, tap)
-            if 3 <= i < 3 + NCT:
-                prep_xb(0, i - 3)
-            if i == 6:
+            c_late = c_at[i]
+            for c in c_at[i]:
+                transposes_c(c, 0)
+                transposes_c(c, 1)
+                copy_c(c, 0)
+                copy_c(c, 1)
+            if pe_tile(i):
+                ev_d(i)
+            if pe_tile(i + 2) and i + 2 < n_a - 2:
+                make_dg(i + 2)
+            dw(i, TAPS[5:8])
+            if 4 <= i < 4 + NCT:
+                prep_xb(0, i - 4)
+            if i == 8:
                 regroup_x(1, "ss")
+            if i == 9:
                 q_x(1)
                 prep_k2(1)
-            dw(i)
+            if i in e_at:
+                ct = e_at[i]
+                fin_half(0, ct, 0)
+                fin_half(0, ct, 1)
+                if ct == NCT - 1:
+                    nc.sync.dma_start(out=outv[0], in_=ot[0][:])
             if t == 3:
-                clip_q(b, s0, 0, NPIX)
-            if 13 <= i < 13 + NCT:
-                fin_half(0, i - 13, 0)
-                fin_half(0, i - 13, 1)
-            if i == 13 + NCT:
-                nc.sync.dma_start(out=outv[0], in_=ot[0][:])
-            if 17 <= i < 17 + NCT:
-                prep_xb(1, i - 17)
+                clip(b, s0, 0, NPIX)
+                h2_at[i + 1] = (b, s0)
+            if i == n_a - 3:
+                mm_a(i + 2)
+                ev_relu(i + 2)
+                ev_clip(i + 2)
+                ev_columns(i + 2)
+                ev_centre(i + 2)
+                ev_rows(i + 2)
+            if i >= 19:
+                prep_xb(1, i - 19)
+        prep_xb(1, 3)
+        for c in c_late:
+            q_c(c)
 
-        for tap in (6, 7, 8):
-            mm_d(n_a - 4, tap)
-        ev_d(n_a - 4)
-
+        for i in (n_a - 2, n_a - 1):
+            make_dg(i)
+            mm_d(i)
+            ev_d(i)
         for ct in range(NCT):
-            pool = pse if ct < 2 else psa
-            e3_t[(1, ct)] = pool.tile([P, NPIX], F32, name="e3" if ct < 2 else "a1")
+            pool = pse if ct == 0 else pst
+            e3_t[(1, ct)] = pool.tile([P, NPIX], F32, name="e3" if ct == 0 else "tp")
         ot[1] = opool.tile([P, NCT, NPIX], F32, name="ot")
         for f_ in range(2):
             pis = [f_, 2 + f_]
             for tap in TAPS:
                 for pi in pis:
-                    stt(n_a - 2, pi, tap)
-                    stt(n_a - 1, pi, tap)
+                    for i in (n_a - 2, n_a - 1):
+                        if pi in vector_patches(i):
+                            stt(i, pi, tap)
             for pi in pis:
-                clip_q(1, 2, pi * P, P)
+                clip(1, 2, pi * P, P)
+            for pi in pis:
+                q_h(1, 2, pi * P, P)
                 for ct in range(NCT):
                     mm_e(1, ct, [pi])
         for f_ in range(2):
             for ct in range(NCT):
                 for pi in (f_, 2 + f_):
                     fin_patch(1, ct, pi)
-            rows = slice(f_ * 256, (f_ + 1) * 256)
-            nc.sync.dma_start(out=outv[1][:, :, rows], in_=ot[1][:, :, rows])
+                if ct % 2 == 1:
+                    cts, rows = slice(ct - 1, ct + 1), slice(f_ * 256, (f_ + 1) * 256)
+                    nc.sync.dma_start(out=outv[1][:, cts, rows], in_=ot[1][:, cts, rows])

@@ -22,6 +22,7 @@ NJ = HID // P
 NCT = C // P
 PE_PATCH = 3
 PE_FIRST = 4
+W3_TWICE = 10
 CENTRE = 4
 TAPS = [3, 5, 0, 1, 2, 6, 7, 8]
 FLOPS = 2 * B * NPIX * (2 * HID * C + 9 * HID)
@@ -353,7 +354,7 @@ def tile_hyperpatchinvertedresidual_kernel(
         h2s = [const.tile([P, 3, NPIX], U8, name="h2s%d" % b, align_bytes=64) for b in range(B)]
 
         def pe_tile(i):
-            return i >= n_a - 2 or (i >= PE_FIRST and (i - PE_FIRST) % 3 == 0 and i < n_a - 3)
+            return i >= n_a - 2 or (i >= PE_FIRST and (i - PE_FIRST) % 4 == 0 and i < n_a - 3)
 
         def vector_patches(i):
             return [pi for pi in range(4) if not (pe_tile(i) and pi == PE_PATCH)]
@@ -409,7 +410,8 @@ def tile_hyperpatchinvertedresidual_kernel(
             acc = acc_t[(b, s0)]
             h2g = hgpool.tile([P, n, 4], BF16, name="h2g", align_bytes=64)
             nc.vector.tensor_scalar(
-                out=h2g[:], in0=acc[:, :, lo : lo + n].rearrange("p t n -> p n t"),
+                out=h2g[:].rearrange("p (c i) t -> p c t i", i=4),
+                in0=acc[:, :, lo : lo + n].rearrange("p t (c i) -> p c t i", i=4),
                 scalar1=0.0, scalar2=6.0, op0=ALU.max, op1=ALU.min,
             )
             h2g_t[(b, s0, lo)] = h2g
@@ -483,10 +485,10 @@ def tile_hyperpatchinvertedresidual_kernel(
 
         c_at = {0: []}
         nxt = 0
-        for i in range(1, n_a - 2):
+        for i in range(1, n_a):
             c_at[i] = [nxt]
             nxt += 1
-            if i in (6, 11, 16):
+            if i == W3_TWICE:
                 c_at[i].append(nxt)
                 nxt += 1
         e_at = {14: 0, 15: 1, 17: 2, 18: 3}
@@ -571,6 +573,12 @@ def tile_hyperpatchinvertedresidual_kernel(
             if i >= 19:
                 prep_xb(1, i - 19)
         prep_xb(1, 3)
+        for i in (n_a - 2, n_a - 1):
+            for c in c_at[i]:
+                transposes_c(c, 0)
+                transposes_c(c, 1)
+                copy_c(c, 0)
+                copy_c(c, 1)
         for c in c_late:
             q_c(c)
 
@@ -589,6 +597,10 @@ def tile_hyperpatchinvertedresidual_kernel(
                     for i in (n_a - 2, n_a - 1):
                         if pi in vector_patches(i):
                             stt(i, pi, tap)
+                if f_ == 0 and tap == TAPS[4]:
+                    for i in (n_a - 2, n_a - 1):
+                        for c in c_at[i]:
+                            q_c(c)
             for pi in pis:
                 clip(1, 2, pi * P, P)
             for pi in pis:

@@ -74,10 +74,12 @@ def tile_hyperpatchinvertedresidual_kernel(
         t1_tiles = {}
         t3_tiles = {}
 
-        def ld_a(i):
+        def ld_a(i, parts=1):
             b, s0, t = a_order[i]
             t1 = raw1.tile([P, 4, 512], BF16, name="t1")
-            nc.sync.dma_start(out=t1[:], in_=w1v[b][:, 3 * t + s0])
+            for part in range(parts):
+                rows = slice(part * 4 // parts, (part + 1) * 4 // parts)
+                nc.sync.dma_start(out=t1[:, rows], in_=w1v[b][:, 3 * t + s0, rows])
             t1_tiles[i] = t1
 
         def ld_c(k):
@@ -102,7 +104,7 @@ def tile_hyperpatchinvertedresidual_kernel(
             eng.dma_start(out=dst[r0 : r0 + 4, :], in_=vec.rearrange("(r e) -> r e", r=4))
 
         k2raw = [const.tile([P, NJ, 36], BF16, name="k2raw%d" % b) for b in range(B)]
-        ld_a(0)
+        ld_a(0, 2)
         ld_vec(nc.scalar, praw, g1, 0)
         ld_vec(nc.scalar, praw, v1, 24)
         ld_vec(nc.scalar, praw, m1, 16)
@@ -331,8 +333,10 @@ def tile_hyperpatchinvertedresidual_kernel(
             )
 
         def ev_columns(i):
-            hp = hp_t[i]
-            nc.scalar.copy(out=hp[:, 1 : H + 1, 0 : WD + 2 : WD + 1], in_=hp[:, 1 : H + 1, 2:WD:29])
+            nc.scalar.activation(
+                out=hp_t[i][:, 1 : H + 1, 0 : WD + 2 : WD + 1],
+                in_=r1_t[i][:, :, 1 : WD - 1 : WD - 3], func=ACT.Relu, bias=six[:], scale=-1.0,
+            )
 
         def ev_rows(i):
             hp = hp_t[i]
@@ -401,7 +405,10 @@ def tile_hyperpatchinvertedresidual_kernel(
 
         def dw(i, taps):
             for tap in taps:
-                for pi in vector_patches(i):
+                pis = vector_patches(i)
+                if TAPS.index(tap) % 2 == 1:
+                    pis = [pis[k] for k in (1, 0, 3, 2) if k < len(pis)]
+                for pi in pis:
                     stt(i, pi, tap)
 
         h2g_t = {}
@@ -529,11 +536,9 @@ def tile_hyperpatchinvertedresidual_kernel(
             dw(i, TAPS[1:3])
             if i == 3:
                 bn_second("c", NCT, inv3, beta3)
-            if more and i > 0:
-                q_a(i + 2)
             dw(i, TAPS[3:5])
-            if i == 0:
-                q_a(2)
+            if more:
+                q_a(i + 2)
             for c in c_late:
                 q_c(c)
             c_late = c_at[i]

@@ -20,7 +20,6 @@ N1, N2, N3 = HID * C, HID * 9, C * HID
 EPS = 1e-5
 NJ = HID // P
 NCT = C // P
-PE_PATCH = 3
 PE_FIRST = 4
 W3_TWICE = 10
 CENTRE = 4
@@ -95,6 +94,8 @@ def tile_hyperpatchinvertedresidual_kernel(
 
         six = const.tile([P, 1], F32, name="six")
         nc.vector.memset(six[:], 6.0)
+        eps = const.tile([P, 1], F32, name="eps")
+        nc.vector.memset(eps[:], EPS)
         praw = const.tile([P, 3 * P], BF16, name="praw")
         nc.vector.memset(praw[:], 0.0)
         praw3 = const.tile([P, P], BF16, name="praw3")
@@ -136,7 +137,6 @@ def tile_hyperpatchinvertedresidual_kernel(
         beta = const.tile([P, 24], F32, name="beta")
         inv3 = const.tile([P, NCT], F32, name="inv3")
         beta3 = const.tile([P, NCT], F32, name="beta3")
-        ninv2 = const.tile([P, NJ], F32, name="ninv2")
         bn_tmp = {}
 
         def bn_first(key, src, n, pool, tag):
@@ -148,26 +148,30 @@ def tile_hyperpatchinvertedresidual_kernel(
                     ptp[:, s * P : (s + 1) * P], src[:, s * P : (s + 1) * P], ident[:]
                 )
             pf = const.tile([P, 4 * n], F32, name="pf" + key)
-            ve = const.tile([P, n], F32, name="ve" + key)
             sd = const.tile([P, n], F32, name="sd" + key)
-            nc.vector.tensor_copy(
-                out=pf[:].rearrange("p (x s) -> p x s", s=blocks),
-                in_=ptp[:, 0 : blocks * P].rearrange("p (s x) -> p x s", s=blocks)[:, 0:rows, :],
+            vectors = ptp[:, 0 : blocks * P].rearrange("p (s x) -> p x s", s=blocks)
+            nc.scalar.activation(
+                out=sd[:].rearrange("p (x s) -> p x s", s=blocks),
+                in_=vectors[:, 3 * rows // 4 : rows, :], func=ACT.Sqrt, bias=eps[:], scale=1.0,
             )
-            bn_tmp[key] = (pf, ve, sd)
+            nc.vector.tensor_copy(
+                out=pf[:].rearrange("p (x s) -> p x s", s=blocks), in_=vectors[:, 0:rows, :]
+            )
+            bn_tmp[key] = (pf, sd)
 
-        def bn_variance(key, n):
-            pf, ve, sd = bn_tmp[key]
-            nc.vector.tensor_scalar_add(out=ve[:], in0=pf[:, 3 * n : 4 * n], scalar1=EPS)
-            nc.scalar.sqrt(out=sd[:], in_=ve[:])
-
-        def bn_second(key, n, inv_o, beta_o):
-            pf, ve, sd = bn_tmp[key]
+        def bn_second(key, n):
+            pf, sd = bn_tmp[key]
+            mg = const.tile([P, n], F32, name="mg" + key)
             rsd = const.tile([P, n], F32, name="rsd" + key)
-            mi = const.tile([P, n], F32, name="mi" + key)
             nc.vector.reciprocal(out=rsd[:], in_=sd[:])
+            nc.vector.tensor_mul(out=mg[:], in0=pf[:, 2 * n : 3 * n], in1=pf[:, 0:n])
+            bn_tmp[key] = (pf, rsd, mg)
+
+        def bn_third(key, n, inv_o, beta_o):
+            pf, rsd, mg = bn_tmp[key]
+            mi = const.tile([P, n], F32, name="mi" + key)
             nc.vector.tensor_mul(out=inv_o[:], in0=pf[:, 0:n], in1=rsd[:])
-            nc.vector.tensor_mul(out=mi[:], in0=pf[:, 2 * n : 3 * n], in1=inv_o[:])
+            nc.vector.tensor_mul(out=mi[:], in0=mg[:], in1=rsd[:])
             nc.vector.tensor_sub(out=beta_o[:], in0=pf[:, n : 2 * n], in1=mi[:])
 
         xc = [const.tile([P, NPIX], U32, name="xc%d" % b, align_bytes=64) for b in range(B)]
@@ -175,16 +179,15 @@ def tile_hyperpatchinvertedresidual_kernel(
         xb = {}
         xg_t = {}
 
-        def regroup_x(b, engs):
-            xg = grp.tile([P, 2048], BF16, name="g", align_bytes=64)
-            xgv = xg[:].rearrange("p (g y z t) -> p g y z t", g=2, y=H, z=16)
+        def regroup_x(b, eng, g_):
+            if g_ == 0:
+                xg_t[b] = grp.tile([P, 2048], BF16, name="g", align_bytes=64)
+            xgv = xg_t[b][:].rearrange("p (g y z t) -> p g y z t", g=2, y=H, z=16)
             xrv = xraw[b][:].rearrange("p t (y g z) -> p g y z t", y=H, g=2)
-            for g_ in range(2):
-                if engs[g_] == "v":
-                    nc.vector.tensor_copy(out=xgv[:, g_], in_=xrv[:, g_])
-                else:
-                    nc.scalar.copy(out=xgv[:, g_], in_=xrv[:, g_])
-            xg_t[b] = xg
+            if eng == "v":
+                nc.vector.tensor_copy(out=xgv[:, g_], in_=xrv[:, g_])
+            else:
+                nc.scalar.copy(out=xgv[:, g_], in_=xrv[:, g_])
 
         def q_x(b):
             nc.vector.quantize_mx(out=xc[b][:].bitcast(FP8X4), scales=xs[b][:], in_=xg_t[b][:])
@@ -201,15 +204,20 @@ def tile_hyperpatchinvertedresidual_kernel(
         ksum = [const.tile([P, NJ, 4], F32, name="ksum%d" % b) for b in range(B)]
         bias2 = [const.tile([P, NJ, 4], F32, name="bias2%d" % b) for b in range(B)]
 
-        def prep_k2(b):
-            nc.vector.tensor_tensor(
-                out=k2f[b][:], in0=k2raw[b][:],
-                in1=ninv2[:].unsqueeze(2).to_broadcast([P, NJ, 36]), op=ALU.mult,
+        def scale_k2(b):
+            nc.vector.scalar_tensor_tensor(
+                out=k2f[b][:], in0=k2raw[b][:], scalar=-1.0,
+                in1=inv[:, 12:24].unsqueeze(2).to_broadcast([P, NJ, 36]),
+                op0=ALU.mult, op1=ALU.mult,
             )
+
+        def sum_k2(b):
             nc.vector.tensor_reduce(
                 out=ksum[b][:], in_=k2f[b][:].rearrange("p j (t e) -> p j e t", e=4),
                 axis=AX.X, op=ALU.add,
             )
+
+        def bias_k2(b):
             nc.vector.scalar_tensor_tensor(
                 out=bias2[b][:], in0=ksum[b][:], scalar=-6.0,
                 in1=beta[:, 12:24].unsqueeze(2).to_broadcast([P, NJ, 4]),
@@ -360,8 +368,11 @@ def tile_hyperpatchinvertedresidual_kernel(
         def pe_tile(i):
             return i >= n_a - 2 or (i >= PE_FIRST and (i - PE_FIRST) % 4 == 0 and i < n_a - 3)
 
+        def pe_patch(i):
+            return 2 if i == n_a - 2 else 3
+
         def vector_patches(i):
-            return [pi for pi in range(4) if not (pe_tile(i) and pi == PE_PATCH)]
+            return [pi for pi in range(4) if not (pe_tile(i) and pi == pe_patch(i))]
 
         dg_t = {}
         d_t = {}
@@ -370,7 +381,7 @@ def tile_hyperpatchinvertedresidual_kernel(
             b, s0, t = a_order[i]
             dg_t[i] = dpool.tile([P, 9, P], F32, name="dg")
             for tap in range(9):
-                k = 4 * tap + fg_of(PE_PATCH)
+                k = 4 * tap + fg_of(pe_patch(i))
                 nc.scalar.activation(
                     out=dg_t[i][:, tap, :], in_=identf[:], func=ACT.Copy,
                     scale=k2f[b][:, 3 * t + s0, k : k + 1],
@@ -381,15 +392,15 @@ def tile_hyperpatchinvertedresidual_kernel(
             for tap in range(9):
                 nc.tensor.matmul(
                     d_t[i][:, 0:P].rearrange("p (y z) -> p y z", y=8),
-                    lhsT=dg_t[i][:, tap, :], rhs=win(hp_t[i], PE_PATCH, tap // 3, tap % 3),
+                    lhsT=dg_t[i][:, tap, :], rhs=win(hp_t[i], pe_patch(i), tap // 3, tap % 3),
                     start=(tap == 0), stop=(tap == 8),
                 )
 
         def ev_d(i):
             b, s0, t = a_order[i]
-            fg = fg_of(PE_PATCH)
+            fg = fg_of(pe_patch(i))
             nc.scalar.activation(
-                out=acc_t[(b, s0)][:, t, PE_PATCH * P : (PE_PATCH + 1) * P], in_=d_t[i][:, 0:P],
+                out=acc_t[(b, s0)][:, t, pe_patch(i) * P : (pe_patch(i) + 1) * P], in_=d_t[i][:, 0:P],
                 func=ACT.Identity, bias=bias2[b][:, 3 * t + s0, fg : fg + 1], scale=1.0,
             )
 
@@ -405,10 +416,7 @@ def tile_hyperpatchinvertedresidual_kernel(
 
         def dw(i, taps):
             for tap in taps:
-                pis = vector_patches(i)
-                if TAPS.index(tap) % 2 == 1:
-                    pis = [pis[k] for k in (1, 0, 3, 2) if k < len(pis)]
-                for pi in pis:
+                for pi in vector_patches(i):
                     stt(i, pi, tap)
 
         h2g_t = {}
@@ -472,23 +480,25 @@ def tile_hyperpatchinvertedresidual_kernel(
 
         t_a(0, 0, "s")
         t_a(0, 1, "v")
-        regroup_x(0, "vs")
+        regroup_x(0, "s", 0)
         bn_first("a", praw, 24, pst, "tp")
+        regroup_x(0, "v", 1)
         t_a(1, 0)
         q_a(0)
-        bn_variance("a", 24)
+        bn_second("a", 24)
         t_a(1, 1)
         q_x(0)
-        bn_second("a", 24, inv, beta)
-        nc.vector.tensor_scalar_mul(out=ninv2[:], in0=inv[:, 12:24], scalar1=-1.0)
+        bn_third("a", 24, inv, beta)
         mm_a(0)
         ev_relu(0)
-        prep_k2(0)
+        scale_k2(0)
+        q_a(1)
+        sum_k2(0)
+        bias_k2(0)
         ev_clip(0)
         ev_columns(0)
         ev_centre(0)
         ev_rows(0)
-        q_a(1)
 
         c_at = {0: []}
         nxt = 0
@@ -511,7 +521,7 @@ def tile_hyperpatchinvertedresidual_kernel(
                 t_a(i + 2, 0)
             dw(i, TAPS[0:1])
             if i in h2_at:
-                q_h(*h2_at[i], 0, NPIX)
+                clip(*h2_at[i], 0, NPIX)
             if more:
                 transposes_a(i + 2, 1)
             mm_a(i + 1)
@@ -532,10 +542,13 @@ def tile_hyperpatchinvertedresidual_kernel(
             ev_rows(i + 1)
             if i == 2:
                 bn_first("c", praw3, NCT, psd, "d")
-                bn_variance("c", NCT)
             dw(i, TAPS[1:3])
+            if i in h2_at:
+                q_h(*h2_at[i], 0, NPIX)
             if i == 3:
-                bn_second("c", NCT, inv3, beta3)
+                bn_second("c", NCT)
+            if i == 4:
+                bn_third("c", NCT, inv3, beta3)
             dw(i, TAPS[3:5])
             if more:
                 q_a(i + 2)
@@ -549,16 +562,20 @@ def tile_hyperpatchinvertedresidual_kernel(
                 copy_c(c, 1)
             if pe_tile(i):
                 ev_d(i)
-            if pe_tile(i + 2) and i + 2 < n_a - 2:
+            if pe_tile(i + 2) and i + 2 < n_a - 1:
                 make_dg(i + 2)
             dw(i, TAPS[5:8])
             if 4 <= i < 4 + NCT:
                 prep_xb(0, i - 4)
             if i == 8:
-                regroup_x(1, "ss")
+                regroup_x(1, "s", 0)
+                regroup_x(1, "s", 1)
             if i == 9:
+                scale_k2(1)
                 q_x(1)
-                prep_k2(1)
+                sum_k2(1)
+            if i == 10:
+                bias_k2(1)
             if i in e_at:
                 ct = e_at[i]
                 fin_half(0, ct, 0)
@@ -566,9 +583,11 @@ def tile_hyperpatchinvertedresidual_kernel(
                 if ct == NCT - 1:
                     nc.sync.dma_start(out=outv[0], in_=ot[0][:])
             if t == 3:
-                clip(b, s0, 0, NPIX)
                 h2_at[i + 1] = (b, s0)
             if i == n_a - 3:
+                for c in c_at[i + 1]:
+                    transposes_c(c, 0)
+                    transposes_c(c, 1)
                 mm_a(i + 2)
                 ev_relu(i + 2)
                 ev_clip(i + 2)
@@ -578,19 +597,23 @@ def tile_hyperpatchinvertedresidual_kernel(
             if i >= 19:
                 prep_xb(1, i - 19)
         prep_xb(1, 3)
-        for i in (n_a - 2, n_a - 1):
-            for c in c_at[i]:
-                transposes_c(c, 0)
-                transposes_c(c, 1)
-                copy_c(c, 0)
-                copy_c(c, 1)
+        mm_d(n_a - 2)
+        for c in c_at[n_a - 2]:
+            copy_c(c, 0)
+            copy_c(c, 1)
+        make_dg(n_a - 1)
+        for c in c_at[n_a - 1]:
+            transposes_c(c, 0)
+            transposes_c(c, 1)
+        ev_d(n_a - 2)
+        for c in c_at[n_a - 1]:
+            copy_c(c, 0)
+            copy_c(c, 1)
+        mm_d(n_a - 1)
+        ev_d(n_a - 1)
         for c in c_late:
             q_c(c)
 
-        for i in (n_a - 2, n_a - 1):
-            make_dg(i)
-            mm_d(i)
-            ev_d(i)
         for ct in range(NCT):
             pool = pse if ct == 0 else pst
             e3_t[(1, ct)] = pool.tile([P, NPIX], F32, name="e3" if ct == 0 else "tp")
@@ -602,8 +625,8 @@ def tile_hyperpatchinvertedresidual_kernel(
                     for i in (n_a - 2, n_a - 1):
                         if pi in vector_patches(i):
                             stt(i, pi, tap)
-                if f_ == 0 and tap == TAPS[4]:
-                    for i in (n_a - 2, n_a - 1):
+                for n, i in enumerate((n_a - 2, n_a - 1)):
+                    if f_ == 0 and tap == TAPS[5 + 2 * n]:
                         for c in c_at[i]:
                             q_c(c)
             for pi in pis:

@@ -36,14 +36,14 @@ def tile_hyperpatchinvertedresidual_kernel(
         const = ctx.enter_context(tc.tile_pool(name="const", bufs=1))
         raw1 = ctx.enter_context(tc.tile_pool(name="raw1", bufs=4))
         raw3 = ctx.enter_context(tc.tile_pool(name="raw3", bufs=2))
-        grp = ctx.enter_context(tc.tile_pool(name="grp", bufs=6))
+        grp = ctx.enter_context(tc.tile_pool(name="grp", bufs=5))
         w1q = ctx.enter_context(tc.tile_pool(name="w1q", bufs=4))
         dpool = ctx.enter_context(tc.tile_pool(name="dpool", bufs=2))
         rpool = ctx.enter_context(tc.tile_pool(name="rpool", bufs=2))
         hpool = ctx.enter_context(tc.tile_pool(name="hpool", bufs=4))
         apool = ctx.enter_context(tc.tile_pool(name="apool", bufs=2))
         hgpool = ctx.enter_context(tc.tile_pool(name="hgpool", bufs=2))
-        xbpool = ctx.enter_context(tc.tile_pool(name="xbpool", bufs=1))
+        xbpool = ctx.enter_context(tc.tile_pool(name="xbpool", bufs=2))
         opool = ctx.enter_context(tc.tile_pool(name="opool", bufs=1))
         pst = ctx.enter_context(tc.psum_pool(name="pst", bufs=5))
         psa = ctx.enter_context(tc.psum_pool(name="psa", bufs=1))
@@ -154,13 +154,13 @@ def tile_hyperpatchinvertedresidual_kernel(
                 out=sd[:].rearrange("p (x s) -> p x s", s=blocks),
                 in_=vectors[:, 3 * rows // 4 : rows, :], func=ACT.Sqrt, bias=eps[:], scale=1.0,
             )
-            nc.vector.tensor_copy(
-                out=pf[:].rearrange("p (x s) -> p x s", s=blocks), in_=vectors[:, 0:rows, :]
-            )
-            bn_tmp[key] = (pf, sd)
+            bn_tmp[key] = (vectors[:, 0:rows, :], pf, sd)
 
         def bn_second(key, n):
-            pf, sd = bn_tmp[key]
+            vectors, pf, sd = bn_tmp[key]
+            nc.vector.tensor_copy(
+                out=pf[:].rearrange("p (x s) -> p x s", s=4 * n // vectors.shape[1]), in_=vectors
+            )
             mg = const.tile([P, n], F32, name="mg" + key)
             rsd = const.tile([P, n], F32, name="rsd" + key)
             nc.vector.reciprocal(out=rsd[:], in_=sd[:])
@@ -441,11 +441,11 @@ def tile_hyperpatchinvertedresidual_kernel(
         ot = {}
         e3_t = {}
 
-        def mm_e(b, ct, pis):
-            e3 = e3_t[(b, ct)]
+        def mm_e(b, ct, pis, s0s=range(3)):
             for pi in pis:
+                e3 = e3_t[(b + (b == 1) * (pi % 2), ct)]
                 cols = slice(pi * P, (pi + 1) * P)
-                for s0 in range(3):
+                for s0 in s0s:
                     u = ct * 3 + s0
                     nc.tensor.matmul_mx(
                         out=e3[:, cols],
@@ -473,7 +473,7 @@ def tile_hyperpatchinvertedresidual_kernel(
 
             nc.vector.scalar_tensor_tensor(
                 out=img(ot[b]),
-                in0=e3_t[(b, ct)][:, pi * P : (pi + 1) * P].rearrange("p (y z) -> p y z", y=8),
+                in0=e3_t[(b + f_, ct)][:, pi * P : (pi + 1) * P].rearrange("p (y z) -> p y z", y=8),
                 scalar=inv3[:, ct : ct + 1], in1=img(xb[b]),
                 op0=ALU.mult, op1=ALU.add,
             )
@@ -485,9 +485,9 @@ def tile_hyperpatchinvertedresidual_kernel(
         regroup_x(0, "v", 1)
         t_a(1, 0)
         q_a(0)
-        bn_second("a", 24)
         t_a(1, 1)
         q_x(0)
+        bn_second("a", 24)
         bn_third("a", 24, inv, beta)
         mm_a(0)
         ev_relu(0)
@@ -508,7 +508,10 @@ def tile_hyperpatchinvertedresidual_kernel(
             if i == W3_TWICE:
                 c_at[i].append(nxt)
                 nxt += 1
-        e_at = {14: 0, 15: 1, 17: 2, 18: 3}
+        e_at = {13: 0, 15: 1, 17: 2, 19: 3}
+        xb_at = [7, 8, 9, 11]
+        dg_at = {max(i - 2, 0): i for i in range(n_a - 2) if pe_tile(i)}
+        dg_at[n_a - 5] = n_a - 2
         h2_at = {}
         c_late = []
 
@@ -562,19 +565,18 @@ def tile_hyperpatchinvertedresidual_kernel(
                 copy_c(c, 1)
             if pe_tile(i):
                 ev_d(i)
-            if pe_tile(i + 2) and i + 2 < n_a - 1:
-                make_dg(i + 2)
+            if i in dg_at:
+                make_dg(dg_at[i])
             dw(i, TAPS[5:8])
-            if 4 <= i < 4 + NCT:
-                prep_xb(0, i - 4)
-            if i == 8:
-                regroup_x(1, "s", 0)
-                regroup_x(1, "s", 1)
-            if i == 9:
+            if i in xb_at:
+                prep_xb(0, xb_at.index(i))
+            if i in (3, 5):
+                regroup_x(1, "s", i // 5)
+            if i == 7:
                 scale_k2(1)
                 q_x(1)
                 sum_k2(1)
-            if i == 10:
+            if i == 8:
                 bias_k2(1)
             if i in e_at:
                 ct = e_at[i]
@@ -594,9 +596,8 @@ def tile_hyperpatchinvertedresidual_kernel(
                 ev_columns(i + 2)
                 ev_centre(i + 2)
                 ev_rows(i + 2)
-            if i >= 19:
-                prep_xb(1, i - 19)
-        prep_xb(1, 3)
+            if i in (13, 14, 15, 17):
+                prep_xb(1, (13, 14, 15, 17).index(i))
         mm_d(n_a - 2)
         for c in c_at[n_a - 2]:
             copy_c(c, 0)
@@ -614,27 +615,33 @@ def tile_hyperpatchinvertedresidual_kernel(
         for c in c_late:
             q_c(c)
 
-        for ct in range(NCT):
-            pool = pse if ct == 0 else pst
-            e3_t[(1, ct)] = pool.tile([P, NPIX], F32, name="e3" if ct == 0 else "tp")
+        banks = [(pse, "e3"), (psa, "a1"), (pst, "tp"), (psd, "d")]
         ot[1] = opool.tile([P, NCT, NPIX], F32, name="ot")
         for f_ in range(2):
             pis = [f_, 2 + f_]
+            for ct in range(NCT):
+                pool, tag = banks[ct] if f_ == 1 else (pst, "tp")
+                e3_t[(1 + f_, ct)] = pool.tile([P, NPIX], F32, name=tag)
             for tap in TAPS:
                 for pi in pis:
                     for i in (n_a - 2, n_a - 1):
                         if pi in vector_patches(i):
                             stt(i, pi, tap)
-                for n, i in enumerate((n_a - 2, n_a - 1)):
-                    if f_ == 0 and tap == TAPS[5 + 2 * n]:
-                        for c in c_at[i]:
-                            q_c(c)
+                if f_ == 0 and tap == TAPS[5]:
+                    for c in c_at[n_a - 2]:
+                        q_c(c)
+            if f_ == 1:
+                for ct in range(NCT):
+                    mm_e(1, ct, pis[0:1], range(2))
             for pi in pis:
                 clip(1, 2, pi * P, P)
+            if f_ == 0:
+                for c in c_at[n_a - 1]:
+                    q_c(c)
             for pi in pis:
                 q_h(1, 2, pi * P, P)
                 for ct in range(NCT):
-                    mm_e(1, ct, [pi])
+                    mm_e(1, ct, [pi], range(2 if pi == 1 else 0, 3))
         for f_ in range(2):
             for ct in range(NCT):
                 for pi in (f_, 2 + f_):

@@ -184,8 +184,11 @@ def tile_hyperpatchinvertedresidual_kernel(
                 xg_t[b] = grp.tile([P, 2048], BF16, name="g", align_bytes=64)
             xgv = xg_t[b][:].rearrange("p (g y z t) -> p g y z t", g=2, y=H, z=16)
             xrv = xraw[b][:].rearrange("p t (y g z) -> p g y z t", y=H, g=2)
-            if eng == "v":
-                nc.vector.tensor_copy(out=xgv[:, g_], in_=xrv[:, g_])
+            if eng == "g":
+                nc.gpsimd.tensor_scalar(
+                    out=xgv[:, g_], in0=xrv[:, g_], scalar1=1.0, scalar2=0.0,
+                    op0=ALU.mult, op1=ALU.add,
+                )
             else:
                 nc.scalar.copy(out=xgv[:, g_], in_=xrv[:, g_])
 
@@ -377,10 +380,11 @@ def tile_hyperpatchinvertedresidual_kernel(
         dg_t = {}
         d_t = {}
 
-        def make_dg(i):
+        def make_dg(i, taps=range(9)):
             b, s0, t = a_order[i]
-            dg_t[i] = dpool.tile([P, 9, P], F32, name="dg")
-            for tap in range(9):
+            if taps[0] == 0:
+                dg_t[i] = dpool.tile([P, 9, P], F32, name="dg")
+            for tap in taps:
                 k = 4 * tap + fg_of(pe_patch(i))
                 nc.scalar.activation(
                     out=dg_t[i][:, tap, :], in_=identf[:], func=ACT.Copy,
@@ -482,7 +486,7 @@ def tile_hyperpatchinvertedresidual_kernel(
         t_a(0, 1, "v")
         regroup_x(0, "s", 0)
         bn_first("a", praw, 24, pst, "tp")
-        regroup_x(0, "v", 1)
+        regroup_x(0, "g", 1)
         t_a(1, 0)
         q_a(0)
         t_a(1, 1)
@@ -492,8 +496,8 @@ def tile_hyperpatchinvertedresidual_kernel(
         mm_a(0)
         ev_relu(0)
         scale_k2(0)
-        q_a(1)
         sum_k2(0)
+        q_a(1)
         bias_k2(0)
         ev_clip(0)
         ev_columns(0)
@@ -510,8 +514,13 @@ def tile_hyperpatchinvertedresidual_kernel(
                 nxt += 1
         e_at = {13: 0, 15: 1, 17: 2, 19: 3}
         xb_at = [7, 8, 9, 11]
-        dg_at = {max(i - 2, 0): i for i in range(n_a - 2) if pe_tile(i)}
-        dg_at[n_a - 5] = n_a - 2
+        dg_at = {}
+        for i in range(n_a - 2):
+            if pe_tile(i):
+                dg_at[i - 3] = (i, range(5))
+                dg_at[i - 2] = (i, range(5, 9))
+        dg_at[n_a - 5] = (n_a - 2, range(5))
+        dg_at[n_a - 4] = (n_a - 2, range(5, 9))
         h2_at = {}
         c_late = []
 
@@ -566,7 +575,7 @@ def tile_hyperpatchinvertedresidual_kernel(
             if pe_tile(i):
                 ev_d(i)
             if i in dg_at:
-                make_dg(dg_at[i])
+                make_dg(*dg_at[i])
             dw(i, TAPS[5:8])
             if i in xb_at:
                 prep_xb(0, xb_at.index(i))
@@ -646,6 +655,7 @@ def tile_hyperpatchinvertedresidual_kernel(
             for ct in range(NCT):
                 for pi in (f_, 2 + f_):
                     fin_patch(1, ct, pi)
-                if ct % 2 == 1:
-                    cts, rows = slice(ct - 1, ct + 1), slice(f_ * 256, (f_ + 1) * 256)
+                if ct % 2 == 1 or (f_ == 1 and ct == 2):
+                    cts = slice(ct - (ct == 1 or f_ == 0), ct + 1)
+                    rows = slice(f_ * 256, (f_ + 1) * 256)
                     nc.sync.dma_start(out=outv[1][:, cts, rows], in_=ot[1][:, cts, rows])

from contextlib import ExitStack

import concourse.mybir as mybir
from concourse.masks import make_identity

FP8X4 = mybir.dt.float8_e4m3fn_x4
BF16 = mybir.dt.bfloat16
F32 = mybir.dt.float32
U32 = mybir.dt.uint32
U8 = mybir.dt.uint8
ACT = mybir.ActivationFunctionType
ALU = mybir.AluOpType
AX = mybir.AxisListType

P = 128
B, C, HID = 2, 512, 1536
H, WD = 16, 32
NPIX = H * WD
N1, N2, N3 = HID * C, HID * 9, C * HID
EPS = 1e-5
NJ = HID // P
NCT = C // P
PE_FIRST = 4
W3_TWICE = 10
CENTRE = 4
TAPS = [3, 5, 0, 1, 2, 6, 7, 8]
FLOPS = 2 * B * NPIX * (2 * HID * C + 9 * HID)


def tile_hyperpatchinvertedresidual_kernel(
    tc, x, w, g1, b1, m1, v1, g2, b2, m2, v2, g3, b3, m3, v3, out
):
    nc = tc.nc
    with ExitStack() as ctx:
        ctx.enter_context(tc.manual_schedule())
        const = ctx.enter_context(tc.tile_pool(name="const", bufs=1))
        raw1 = ctx.enter_context(tc.tile_pool(name="raw1", bufs=4))
        raw3 = ctx.enter_context(tc.tile_pool(name="raw3", bufs=2))
        grp = ctx.enter_context(tc.tile_pool(name="grp", bufs=5))
        w1q = ctx.enter_context(tc.tile_pool(name="w1q", bufs=4))
        dpool = ctx.enter_context(tc.tile_pool(name="dpool", bufs=2))
        rpool = ctx.enter_context(tc.tile_pool(name="rpool", bufs=2))
        hpool = ctx.enter_context(tc.tile_pool(name="hpool", bufs=4))
        apool = ctx.enter_context(tc.tile_pool(name="apool", bufs=2))
        hgpool = ctx.enter_context(tc.tile_pool(name="hgpool", bufs=2))
        xbpool = ctx.enter_context(tc.tile_pool(name="xbpool", bufs=2))
        opool = ctx.enter_context(tc.tile_pool(name="opool", bufs=1))
        pst = ctx.enter_context(tc.psum_pool(name="pst", bufs=5))
        psa = ctx.enter_context(tc.psum_pool(name="psa", bufs=1))
        pse = ctx.enter_context(tc.psum_pool(name="pse", bufs=1))
        psd = ctx.enter_context(tc.psum_pool(name="psd", bufs=1))

        w1v = [
            w[b, 0:N1].rearrange("(j a q c) f g -> q j a (c f g)", j=NJ, a=4, q=P)
            for b in range(B)
        ]
        w3v = [
            w[b, N1 + N2 : N1 + N2 + N3].rearrange(
                "(m q s o) f g -> q m (s o f g)", m=16, q=P, s=3
            )
            for b in range(B)
        ]
        k2v = [
            w[b, N1 : N1 + N2].rearrange("(j p t) f g -> p j (t f g)", p=P, t=9)
            for b in range(B)
        ]
        outv = [out[b].rearrange("(ct p) y z -> p ct (y z)", p=P) for b in range(B)]

        a_order = [(b, s0, t) for b in range(B) for s0 in range(3) for t in range(4)]
        c_order = [(b, ct, s0) for b in range(B) for ct in range(NCT) for s0 in range(3)]
        n_a = len(a_order)

        t1_tiles = {}
        t3_tiles = {}

        def ld_a(i, parts=1):
            b, s0, t = a_order[i]
            t1 = raw1.tile([P, 4, 512], BF16, name="t1")
            for part in range(parts):
                rows = slice(part * 4 // parts, (part + 1) * 4 // parts)
                nc.sync.dma_start(out=t1[:, rows], in_=w1v[b][:, 3 * t + s0, rows])
            t1_tiles[i] = t1

        def ld_c(k):
            b, ct = k // NCT, k % NCT
            t3 = raw3.tile([P, 4, 1536], BF16, name="t3")
            nc.sync.dma_start(out=t3[:], in_=w3v[b][:, 4 * ct : 4 * ct + 4])
            t3_tiles[k] = t3

        xraw = [const.tile([P, 4, NPIX], BF16, name="xraw%d" % b) for b in range(B)]

        def ld_x(b):
            nc.sync.dma_start(out=xraw[b][:], in_=x[b].rearrange("(t p) y z -> p t (y z)", p=P))

        six = const.tile([P, 1], F32, name="six")
        nc.vector.memset(six[:], 6.0)
        eps = const.tile([P, 1], F32, name="eps")
        nc.vector.memset(eps[:], EPS)
        praw = const.tile([P, 3 * P], BF16, name="praw")
        nc.vector.memset(praw[:], 0.0)
        praw3 = const.tile([P, P], BF16, name="praw3")
        nc.vector.memset(praw3[:], 0.0)

        def ld_vec(eng, dst, vec, r0):
            eng.dma_start(out=dst[r0 : r0 + 4, :], in_=vec.rearrange("(r e) -> r e", r=4))

        k2raw = [const.tile([P, NJ, 36], BF16, name="k2raw%d" % b) for b in range(B)]
        ld_a(0, 2)
        ld_vec(nc.scalar, praw, g1, 0)
        ld_vec(nc.scalar, praw, v1, 24)
        ld_vec(nc.scalar, praw, m1, 16)
        ld_vec(nc.scalar, praw, b1, 8)
        ld_x(0)
        ld_vec(nc.sync, praw, g2, 4)
        ld_vec(nc.sync, praw, v2, 28)
        ld_vec(nc.sync, praw, m2, 20)
        ld_vec(nc.sync, praw, b2, 12)
        identf = const.tile([P, P], F32, name="identf")
        make_identity(nc, identf[:])
        ident = const.tile([P, P], BF16, name="ident")
        make_identity(nc, ident[:])
        ld_a(1)
        nc.sync.dma_start(out=k2raw[0][:], in_=k2v[0])
        ld_a(2)
        ld_a(3)
        ld_c(0)
        ld_x(1)
        ld_vec(nc.sync, praw3, g3, 0)
        ld_vec(nc.sync, praw3, v3, 12)
        ld_vec(nc.sync, praw3, m3, 8)
        ld_vec(nc.sync, praw3, b3, 4)
        nc.sync.dma_start(out=k2raw[1][:], in_=k2v[1])
        warm = const.tile([P, 1], F32, name="warm")
        nc.scalar.sqrt(out=warm[:], in_=six[:])

        inv = const.tile([P, 24], F32, name="inv")
        beta = const.tile([P, 24], F32, name="beta")
        inv3 = const.tile([P, NCT], F32, name="inv3")
        beta3 = const.tile([P, NCT], F32, name="beta3")
        bn_tmp = {}

        def bn_first(key, src, n, pool, tag):
            rows = 4 * n * P // src.shape[1]
            blocks = src.shape[1] // P
            ptp = pool.tile([P, 1024], BF16, name=tag)
            for s in range(blocks):
                nc.tensor.transpose(
                    ptp[:, s * P : (s + 1) * P], src[:, s * P : (s + 1) * P], ident[:]
                )
            pf = const.tile([P, 4 * n], F32, name="pf" + key)
            sd = const.tile([P, n], F32, name="sd" + key)
            vectors = ptp[:, 0 : blocks * P].rearrange("p (s x) -> p x s", s=blocks)
            nc.scalar.activation(
                out=sd[:].rearrange("p (x s) -> p x s", s=blocks),
                in_=vectors[:, 3 * rows // 4 : rows, :], func=ACT.Sqrt, bias=eps[:], scale=1.0,
            )
            bn_tmp[key] = (vectors[:, 0:rows, :], pf, sd)

        def bn_second(key, n):
            vectors, pf, sd = bn_tmp[key]
            nc.vector.tensor_copy(
                out=pf[:].rearrange("p (x s) -> p x s", s=4 * n // vectors.shape[1]), in_=vectors
            )
            mg = const.tile([P, n], F32, name="mg" + key)
            rsd = const.tile([P, n], F32, name="rsd" + key)
            nc.vector.reciprocal(out=rsd[:], in_=sd[:])
            nc.vector.tensor_mul(out=mg[:], in0=pf[:, 2 * n : 3 * n], in1=pf[:, 0:n])
            bn_tmp[key] = (pf, rsd, mg)

        def bn_third(key, n, inv_o, beta_o):
            pf, rsd, mg = bn_tmp[key]
            mi = const.tile([P, n], F32, name="mi" + key)
            nc.vector.tensor_mul(out=inv_o[:], in0=pf[:, 0:n], in1=rsd[:])
            nc.vector.tensor_mul(out=mi[:], in0=mg[:], in1=rsd[:])
            nc.vector.tensor_sub(out=beta_o[:], in0=pf[:, n : 2 * n], in1=mi[:])

        xc = [const.tile([P, NPIX], U32, name="xc%d" % b, align_bytes=64) for b in range(B)]
        xs = [const.tile([P, NPIX], U8, name="xs%d" % b, align_bytes=64) for b in range(B)]
        xb = {}
        xg_t = {}

        def regroup_x(b, eng, g_):
            if g_ == 0:
                xg_t[b] = grp.tile([P, 2048], BF16, name="g", align_bytes=64)
            xgv = xg_t[b][:].rearrange("p (g y z t) -> p g y z t", g=2, y=H, z=16)
            xrv = xraw[b][:].rearrange("p t (y g z) -> p g y z t", y=H, g=2)
            if eng == "g":
                nc.gpsimd.tensor_scalar(
                    out=xgv[:, g_], in0=xrv[:, g_], scalar1=1.0, scalar2=0.0,
                    op0=ALU.mult, op1=ALU.add,
                )
            else:
                nc.scalar.copy(out=xgv[:, g_], in_=xrv[:, g_])

        def q_x(b):
            nc.vector.quantize_mx(out=xc[b][:].bitcast(FP8X4), scales=xs[b][:], in_=xg_t[b][:])

        def prep_xb(b, ct):
            if ct == 0:
                xb[b] = xbpool.tile([P, NCT, NPIX], F32, name="xb")
            nc.scalar.activation(
                out=xb[b][:, ct, :], in_=xraw[b][:, ct, :], func=ACT.Identity,
                bias=beta3[:, ct : ct + 1], scale=1.0,
            )

        k2f = [const.tile([P, NJ, 36], F32, name="k2f%d" % b) for b in range(B)]
        ksum = [const.tile([P, NJ, 4], F32, name="ksum%d" % b) for b in range(B)]
        bias2 = [const.tile([P, NJ, 4], F32, name="bias2%d" % b) for b in range(B)]

        def scale_k2(b):
            nc.vector.scalar_tensor_tensor(
                out=k2f[b][:], in0=k2raw[b][:], scalar=-1.0,
                in1=inv[:, 12:24].unsqueeze(2).to_broadcast([P, NJ, 36]),
                op0=ALU.mult, op1=ALU.mult,
            )

        def sum_k2(b):
            nc.vector.tensor_reduce(
                out=ksum[b][:], in_=k2f[b][:].rearrange("p j (t e) -> p j e t", e=4),
                axis=AX.X, op=ALU.add,
            )

        def bias_k2(b):
            nc.vector.scalar_tensor_tensor(
                out=bias2[b][:], in0=ksum[b][:], scalar=-6.0,
                in1=beta[:, 12:24].unsqueeze(2).to_broadcast([P, NJ, 4]),
                op0=ALU.mult, op1=ALU.add,
            )

        def fg_of(pi):
            return 2 * (pi % 2) + pi // 2

        ga_t = {}
        gc_t = {}
        w1c_t = {}
        w1s_t = {}

        tpa_t = {}

        def transposes_a(i, f_):
            t1w = t1_tiles[i][:].bitcast(F32)
            tpa_t[f_] = pst.tile([P, 512], F32, name="tp")
            for a in range(4):
                nc.tensor.transpose(
                    tpa_t[f_][:, a * P : (a + 1) * P], t1w[:, a, f_:256:2], identf[:]
                )

        def copy_a(i, f_, eng="s"):
            if f_ == 0:
                ga_t[i] = grp.tile([P, 2048], BF16, name="g", align_bytes=64)
            dst = ga_t[i][:].rearrange("p (g f n) -> p f g n", g=2, f=2)[:, f_]
            tp = tpa_t[f_]
            src = tp[:].bitcast(BF16).rearrange("p (n g) -> p g n", g=2)
            if eng == "v":
                nc.vector.tensor_copy(out=dst, in_=src)
            else:
                nc.scalar.copy(out=dst, in_=src)

        def t_a(i, f_, eng="s"):
            transposes_a(i, f_)
            copy_a(i, f_, eng)

        def q_a(i):
            w1c = w1q.tile([P, 512], U32, name="w1c", align_bytes=64)
            w1s = w1q.tile([P, 512], U8, name="w1s", align_bytes=64)
            nc.vector.quantize_mx(out=w1c[:].bitcast(FP8X4), scales=w1s[:], in_=ga_t[i][:])
            w1c_t[i], w1s_t[i] = w1c, w1s

        w3c = [const.tile([P, 12, 512], U32, name="w3c%d" % b, align_bytes=64) for b in range(B)]
        w3s = [const.tile([P, 12, 512], U8, name="w3s%d" % b, align_bytes=64) for b in range(B)]

        tpc_t = {}

        def transposes_c(i, half):
            b, ct, s0 = c_order[i]
            k = b * NCT + ct
            if half == 0 and s0 == 0 and k + 1 < B * NCT:
                ld_c(k + 1)
            t3 = t3_tiles[k]
            tp = pst.tile([P, 1024], BF16, name="tp")
            for kk in range(8):
                pi, a = 2 * half + kk // 4, kk % 4
                src = t3[:, a, :].rearrange("q (s o e) -> q s o e", s=3, e=4)[:, s0, :, fg_of(pi)]
                nc.tensor.transpose(tp[:, kk * P : (kk + 1) * P], src, ident[:])
            tpc_t[(i, half)] = tp

        def copy_c(i, half):
            if half == 0:
                gc_t[i] = grp.tile([P, 2048], BF16, name="g", align_bytes=64)
            nc.scalar.copy(
                out=gc_t[i][:, half * 1024 : (half + 1) * 1024], in_=tpc_t[(i, half)][:]
            )

        def q_c(i):
            b, ct, s0 = c_order[i]
            u = ct * 3 + s0
            nc.vector.quantize_mx(
                out=w3c[b][:, u, :].bitcast(FP8X4), scales=w3s[b][:, u, :], in_=gc_t[i][:]
            )

        a1_t = {}
        hp_t = {}
        acc_t = {}

        def win(hp, pi, dy, dx):
            g_, f_ = pi // 2, pi % 2
            return hp[:, 8 * f_ + dy : 8 * f_ + dy + 8, 16 * g_ + dx : 16 * g_ + dx + 16]

        def accv(acc, t, pi):
            return acc[:, t, pi * P : (pi + 1) * P].rearrange("p (y z) -> p y z", y=8)

        def mm_a(i):
            b, s0, t = a_order[i]
            a1 = psa.tile([P, NPIX], F32, name="a1")
            for pi in range(4):
                cols = slice(pi * P, (pi + 1) * P)
                nc.tensor.matmul_mx(
                    out=a1[:, cols],
                    lhsT=w1c_t[i][:, cols].bitcast(FP8X4), lhsT_scale=w1s_t[i][:, cols],
                    rhs=xc[b][:, cols].bitcast(FP8X4), rhs_scale=xs[b][:, cols],
                    start=True, stop=True,
                )
            a1_t[i] = a1

        r1_t = {}

        def inner(i):
            return hp_t[i][:, 1 : H + 1, 1 : WD + 1]

        def ev_relu(i):
            b, s0, t = a_order[i]
            j = 3 * t + s0
            r1_t[i] = rpool.tile([P, H, WD], F32, name="r1")
            nc.scalar.activation(
                out=r1_t[i][:].rearrange("p y (g z) -> p g y z", g=2),
                in_=a1_t[i][:].rearrange("p (g y z) -> p g y z", g=2, y=H),
                func=ACT.Relu, bias=beta[:, j : j + 1], scale=inv[:, j : j + 1],
            )

        def ev_clip(i):
            hp_t[i] = hpool.tile([P, H + 2, WD + 2], F32, name="hp")
            nc.scalar.activation(
                out=inner(i), in_=r1_t[i][:], func=ACT.Relu, bias=six[:], scale=-1.0
            )

        def ev_columns(i):
            nc.scalar.activation(
                out=hp_t[i][:, 1 : H + 1, 0 : WD + 2 : WD + 1],
                in_=r1_t[i][:, :, 1 : WD - 1 : WD - 3], func=ACT.Relu, bias=six[:], scale=-1.0,
            )

        def ev_rows(i):
            hp = hp_t[i]
            nc.scalar.copy(out=hp[:, 0 : H + 2 : H + 1, :], in_=hp[:, 2:H:13, :])

        def ev_centre(i):
            b, s0, t = a_order[i]
            j = 3 * t + s0
            if t == 0:
                acc_t[(b, s0)] = apool.tile([P, 4, NPIX], F32, name="acc")
            for pi in vector_patches(i):
                k = 4 * CENTRE + fg_of(pi)
                nc.scalar.activation(
                    out=accv(acc_t[(b, s0)], t, pi), in_=win(hp_t[i], pi, 1, 1), func=ACT.Identity,
                    bias=bias2[b][:, j, fg_of(pi) : fg_of(pi) + 1], scale=k2f[b][:, j, k : k + 1],
                )

        h2c = [const.tile([P, 3, NPIX], U32, name="h2c%d" % b, align_bytes=64) for b in range(B)]
        h2s = [const.tile([P, 3, NPIX], U8, name="h2s%d" % b, align_bytes=64) for b in range(B)]

        def pe_tile(i):
            return i >= n_a - 2 or (i >= PE_FIRST and (i - PE_FIRST) % 4 == 0 and i < n_a - 3)

        def pe_patch(i):
            return 2 if i == n_a - 2 else 3

        def vector_patches(i):
            return [pi for pi in range(4) if not (pe_tile(i) and pi == pe_patch(i))]

        dg_t = {}
        d_t = {}

        def make_dg(i, taps=range(9)):
            b, s0, t = a_order[i]
            if taps[0] == 0:
                dg_t[i] = dpool.tile([P, 9, P], F32, name="dg")
            for tap in taps:
                k = 4 * tap + fg_of(pe_patch(i))
                nc.scalar.activation(
                    out=dg_t[i][:, tap, :], in_=identf[:], func=ACT.Copy,
                    scale=k2f[b][:, 3 * t + s0, k : k + 1],
                )

        def mm_d(i):
            d_t[i] = psd.tile([P, NPIX], F32, name="d")
            for tap in range(9):
                nc.tensor.matmul(
                    d_t[i][:, 0:P].rearrange("p (y z) -> p y z", y=8),
                    lhsT=dg_t[i][:, tap, :], rhs=win(hp_t[i], pe_patch(i), tap // 3, tap % 3),
                    start=(tap == 0), stop=(tap == 8),
                )

        def ev_d(i):
            b, s0, t = a_order[i]
            fg = fg_of(pe_patch(i))
            nc.scalar.activation(
                out=acc_t[(b, s0)][:, t, pe_patch(i) * P : (pe_patch(i) + 1) * P], in_=d_t[i][:, 0:P],
                func=ACT.Identity, bias=bias2[b][:, 3 * t + s0, fg : fg + 1], scale=1.0,
            )

        def stt(i, pi, tap):
            b, s0, t = a_order[i]
            k = tap * 4 + fg_of(pi)
            acc = acc_t[(b, s0)]
            nc.vector.scalar_tensor_tensor(
                out=accv(acc, t, pi), in0=win(hp_t[i], pi, tap // 3, tap % 3),
                scalar=k2f[b][:, 3 * t + s0, k : k + 1], in1=accv(acc, t, pi),
                op0=ALU.mult, op1=ALU.add,
            )

        def dw(i, taps):
            for tap in taps:
                for pi in vector_patches(i):
                    stt(i, pi, tap)

        h2g_t = {}

        def clip(b, s0, lo, n):
            acc = acc_t[(b, s0)]
            h2g = hgpool.tile([P, n, 4], BF16, name="h2g", align_bytes=64)
            nc.vector.tensor_scalar(
                out=h2g[:].rearrange("p (c i) t -> p c t i", i=4),
                in0=acc[:, :, lo : lo + n].rearrange("p t (c i) -> p c t i", i=4),
                scalar1=0.0, scalar2=6.0, op0=ALU.max, op1=ALU.min,
            )
            h2g_t[(b, s0, lo)] = h2g

        def q_h(b, s0, lo, n):
            h2g = h2g_t[(b, s0, lo)]
            nc.vector.quantize_mx(
                out=h2c[b][:, s0, lo : lo + n].bitcast(FP8X4), scales=h2s[b][:, s0, lo : lo + n],
                in_=h2g[:].rearrange("p n t -> p (n t)"),
            )

        ot = {}
        e3_t = {}

        def mm_e(b, ct, pis, s0s=range(3)):
            for pi in pis:
                e3 = e3_t[(b + (b == 1) * (pi % 2), ct)]
                cols = slice(pi * P, (pi + 1) * P)
                for s0 in s0s:
                    u = ct * 3 + s0
                    nc.tensor.matmul_mx(
                        out=e3[:, cols],
                        lhsT=w3c[b][:, u, cols].bitcast(FP8X4), lhsT_scale=w3s[b][:, u, cols],
                        rhs=h2c[b][:, s0, cols].bitcast(FP8X4), rhs_scale=h2s[b][:, s0, cols],
                        start=(s0 == 0), stop=(s0 == 2),
                    )

        def fin_half(b, ct, g_):
            nc.vector.scalar_tensor_tensor(
                out=ot[b][:, ct, :].rearrange("p (y g z) -> p g y z", y=H, g=2)[:, g_],
                in0=e3_t[(b, ct)][:, g_ * 256 : (g_ + 1) * 256].rearrange("p (y z) -> p y z", y=H),
                scalar=inv3[:, ct : ct + 1],
                in1=xb[b][:, ct, :].rearrange("p (y g z) -> p g y z", y=H, g=2)[:, g_],
                op0=ALU.mult, op1=ALU.add,
            )

        def fin_patch(b, ct, pi):
            g_, f_ = pi // 2, pi % 2

            def img(tl):
                return tl[:, ct, :].rearrange("p (y z) -> p y z", y=H)[
                    :, 8 * f_ : 8 * f_ + 8, 16 * g_ : 16 * g_ + 16
                ]

            nc.vector.scalar_tensor_tensor(
                out=img(ot[b]),
                in0=e3_t[(b + f_, ct)][:, pi * P : (pi + 1) * P].rearrange("p (y z) -> p y z", y=8),
                scalar=inv3[:, ct : ct + 1], in1=img(xb[b]),
                op0=ALU.mult, op1=ALU.add,
            )

        t_a(0, 0, "s")
        t_a(0, 1, "v")
        regroup_x(0, "s", 0)
        bn_first("a", praw, 24, pst, "tp")
        regroup_x(0, "g", 1)
        t_a(1, 0)
        q_a(0)
        t_a(1, 1)
        q_x(0)
        bn_second("a", 24)
        bn_third("a", 24, inv, beta)
        mm_a(0)
        ev_relu(0)
        scale_k2(0)
        sum_k2(0)
        q_a(1)
        bias_k2(0)
        ev_clip(0)
        ev_columns(0)
        ev_centre(0)
        ev_rows(0)

        c_at = {0: []}
        nxt = 0
        for i in range(1, n_a):
            c_at[i] = [nxt]
            nxt += 1
            if i == W3_TWICE:
                c_at[i].append(nxt)
                nxt += 1
        e_at = {13: 0, 15: 1, 17: 2, 19: 3}
        xb_at = [7, 8, 9, 11]
        dg_at = {}
        for i in range(n_a - 2):
            if pe_tile(i):
                dg_at[i - 3] = (i, range(5))
                dg_at[i - 2] = (i, range(5, 9))
        dg_at[n_a - 5] = (n_a - 2, range(5))
        dg_at[n_a - 4] = (n_a - 2, range(5, 9))
        h2_at = {}
        c_late = []

        for i in range(n_a - 2):
            b, s0, t = a_order[i]
            if i + 4 < n_a:
                ld_a(i + 4)
            more = i + 2 < n_a
            if more:
                t_a(i + 2, 0)
            dw(i, TAPS[0:1])
            if i in h2_at:
                clip(*h2_at[i], 0, NPIX)
            if more:
                transposes_a(i + 2, 1)
            mm_a(i + 1)
            if i in e_at:
                ct = e_at[i]
                if ct == 0:
                    ot[0] = opool.tile([P, NCT, NPIX], F32, name="ot")
                e3_t[(0, ct)] = pse.tile([P, NPIX], F32, name="e3")
                mm_e(0, ct, range(4))
            if pe_tile(i):
                mm_d(i)
            ev_relu(i + 1)
            if more:
                copy_a(i + 2, 1)
            ev_clip(i + 1)
            ev_columns(i + 1)
            ev_centre(i + 1)
            ev_rows(i + 1)
            if i == 2:
                bn_first("c", praw3, NCT, psd, "d")
            dw(i, TAPS[1:3])
            if i in h2_at:
                q_h(*h2_at[i], 0, NPIX)
            if i == 3:
                bn_second("c", NCT)
            if i == 4:
                bn_third("c", NCT, inv3, beta3)
            dw(i, TAPS[3:5])
            if more:
                q_a(i + 2)
            for c in c_late:
                q_c(c)
            c_late = c_at[i]
            for c in c_at[i]:
                transposes_c(c, 0)
                transposes_c(c, 1)
                copy_c(c, 0)
                copy_c(c, 1)
            if pe_tile(i):
                ev_d(i)
            if i in dg_at:
                make_dg(*dg_at[i])
            dw(i, TAPS[5:8])
            if i in xb_at:
                prep_xb(0, xb_at.index(i))
            if i in (3, 5):
                regroup_x(1, "s", i // 5)
            if i == 7:
                scale_k2(1)
                q_x(1)
                sum_k2(1)
            if i == 8:
                bias_k2(1)
            if i in e_at:
                ct = e_at[i]
                fin_half(0, ct, 0)
                fin_half(0, ct, 1)
                if ct == NCT - 1:
                    nc.sync.dma_start(out=outv[0], in_=ot[0][:])
            if t == 3:
                h2_at[i + 1] = (b, s0)
            if i == n_a - 3:
                for c in c_at[i + 1]:
                    transposes_c(c, 0)
                    transposes_c(c, 1)
                mm_a(i + 2)
                ev_relu(i + 2)
                ev_clip(i + 2)
                ev_columns(i + 2)
                ev_centre(i + 2)
                ev_rows(i + 2)
            if i in (13, 14, 15, 17):
                prep_xb(1, (13, 14, 15, 17).index(i))
        mm_d(n_a - 2)
        for c in c_at[n_a - 2]:
            copy_c(c, 0)
            copy_c(c, 1)
        make_dg(n_a - 1)
        for c in c_at[n_a - 1]:
            transposes_c(c, 0)
            transposes_c(c, 1)
        ev_d(n_a - 2)
        for c in c_at[n_a - 1]:
            copy_c(c, 0)
            copy_c(c, 1)
        mm_d(n_a - 1)
        ev_d(n_a - 1)
        for c in c_late:
            q_c(c)

        banks = [(pse, "e3"), (psa, "a1"), (pst, "tp"), (psd, "d")]
        ot[1] = opool.tile([P, NCT, NPIX], F32, name="ot")
        for f_ in range(2):
            pis = [f_, 2 + f_]
            for ct in range(NCT):
                pool, tag = banks[ct] if f_ == 1 else (pst, "tp")
                e3_t[(1 + f_, ct)] = pool.tile([P, NPIX], F32, name=tag)
            for tap in TAPS:
                for pi in pis:
                    for i in (n_a - 2, n_a - 1):
                        if pi in vector_patches(i):
                            stt(i, pi, tap)
                if f_ == 0 and tap == TAPS[5]:
                    for c in c_at[n_a - 2]:
                        q_c(c)
            if f_ == 1:
                for ct in range(NCT):
                    mm_e(1, ct, pis[0:1], range(2))
            for pi in pis:
                clip(1, 2, pi * P, P)
            if f_ == 0:
                for c in c_at[n_a - 1]:
                    q_c(c)
            for pi in pis:
                q_h(1, 2, pi * P, P)
                for ct in range(NCT):
                    mm_e(1, ct, [pi], range(2 if pi == 1 else 0, 3))
        for f_ in range(2):
            for ct in range(NCT):
                for pi in (f_, 2 + f_):
                    fin_patch(1, ct, pi)
                if ct % 2 == 1 or (f_ == 1 and ct == 2):
                    cts = slice(ct - (ct == 1 or f_ == 0), ct + 1)
                    rows = slice(f_ * 256, (f_ + 1) * 256)
                    nc.sync.dma_start(out=outv[1][:, cts, rows], in_=ot[1][:, cts, rows])
